import numpy as np
import ml_dtypes


def mxq(x, axis, fmt="e4m3"):
    dtype, down = {"e4m3": (ml_dtypes.float8_e4m3fn, 7), "e5m2": (ml_dtypes.float8_e5m2, 14)}[fmt]
    v = np.moveaxis(np.asarray(x, np.float32).astype(ml_dtypes.bfloat16).astype(np.float64), axis, -1)
    blocks = v.reshape(v.shape[:-1] + (-1, 32))
    amax = np.abs(blocks).max(-1, keepdims=True)
    byte = np.maximum(np.where(amax > 0, np.frexp(amax)[1] - 1 + 127, 0) - down, 1)
    scale = np.exp2(byte - 127.0)
    codes = (blocks / scale).astype(np.float32).astype(dtype).astype(np.float64)
    return np.moveaxis((codes * scale).reshape(v.shape), -1, axis)


WIDE = False


def mx_kscale(k):
    if not WIDE:
        return np.ones(k)
    levels = np.array([10, -10, 5, -5, 0])
    a = np.random.permutation(np.resize(levels, k // 512 * 4)).reshape(k // 512, 4)
    idx = np.arange(k)
    return np.exp2(a[idx // 512, idx % 128 // 32])


BF16 = ml_dtypes.bfloat16


def bf(x):
    return np.asarray(x, np.float32).astype(BF16)


def f64(x):
    return np.asarray(x).astype(np.float64)


B, N, C0, C1, C2, O0, O1, O2 = 16, 16, 512, 512, 512, 512, 2048, 512
P = C0 + C1
K = P + 2 * C2


def sigmoid(v):
    return 1.0 / (1.0 + np.exp(-v))


def setup_inputs():
    s = mx_kscale(K)[:P]
    lo = 0.4 * np.random.random((B, N, 1, C2))
    hi = 1.0 - 0.4 * np.random.random((B, N, 1, C2))
    x2 = lo + (hi - lo) * np.random.random((B, N, N, C2))
    i = np.arange(N)
    x2[:, i, i, :] = np.random.random((B, N, C2)) < 0.5
    w = np.random.standard_normal((K, O1)) * 2.0 / np.sqrt(K)
    w[:P] = w[:P] / s[:, None]
    return {"x0": bf(np.random.random((B, C0)) * s[:C0]),
            "x1": bf(np.random.random((B, N, C1)) * s[C0:]),
            "x2": bf(x2),
            "W1": bf(w),
            "b1": bf(np.random.standard_normal(O1) * 0.3)}


def reference(x0, x1, x2, W1, b1):
    x0, x1, x2 = f64(x0), f64(x1), f64(x2)
    e0 = np.broadcast_to(x0[:, None, :], (B, N, C0))
    diag = np.eye(N, dtype=bool)[None, :, :, None]
    rmax = np.where(diag, 0.0, x2).max(axis=2)
    rmin = np.where(diag, 1.0, x2).min(axis=2)
    f1 = np.concatenate([e0, x1, rmax, rmin], axis=-1)
    return sigmoid((mxq(f1, 2, "e4m3") @ mxq(f64(W1), 0, "e4m3")) + f64(b1))

@@ -1,0 +1,228 @@
+from contextlib import ExitStack
+
+import concourse.mybir as mybir
+from concourse.masks import make_identity
+
+BF16 = mybir.dt.bfloat16
+F32 = mybir.dt.float32
+U32 = mybir.dt.uint32
+U8 = mybir.dt.uint8
+FP8X4 = mybir.dt.float8_e4m3fn_x4
+ALU = mybir.AluOpType
+ACT = mybir.ActivationFunctionType
+
+P = 128
+PACK = 4
+SCENES = 16
+OBJECTS = 16
+CH = 512
+PASSES = 4
+N_OUT = 2048
+N_TILE = 512
+N_TILES = N_OUT // N_TILE
+TOKENS = 2
+SAME_SCENE = P // SCENES
+HALF_J = OBJECTS // 2
+W_PIECES = PASSES * N_TILES
+W_LOADS = W_PIECES // 2
+VECTOR_PIECES = 2
+EXTREMES = (("max", ALU.max), ("min", ALU.min))
+
+FLOPS = 2 * SCENES * OBJECTS * PASSES * CH * N_OUT
+
+
+def tile_differentiablelogicmachine_pb_kernel(tc, x0, x1, x2, W1, b1, out):
+    nc = tc.nc
+    x1_tokens = x1.rearrange("b (s r) c -> (b s) r c", r=TOKENS)
+    x2_tokens = x2.rearrange("b (s r) j c -> (b s) r j c", r=TOKENS)
+    out_tokens = out.rearrange("b (s r) n -> (b s) r n", r=TOKENS)
+    w_rows = W1.rearrange("(c p t) n -> c p t n", p=P, t=PACK)
+
+    with ExitStack() as ctx:
+        keep = ctx.enter_context(tc.tile_pool(name="keep", bufs=1))
+        stage = ctx.enter_context(tc.tile_pool(name="stage", bufs=6))
+        tree = ctx.enter_context(tc.tile_pool(name="tree", bufs=2))
+        results = ctx.enter_context(tc.tile_pool(name="results", bufs=3))
+        psum = ctx.enter_context(tc.psum_pool(name="psum", bufs=1))
+
+        ident = keep.tile([P, P], F32)
+        make_identity(nc, ident[:])
+        warm = keep.tile([P, 1], F32)
+        nc.vector.memset(warm[:], 0.0)
+        nc.scalar.activation(out=warm[:], in_=warm[:], func=ACT.Sigmoid)
+        run = {}
+        for name, fill in (("max", 0.0), ("min", 1.0)):
+            run[name] = keep.tile([P, TOKENS, CH], BF16, name="run_" + name)
+            nc.vector.memset(run[name][:], fill)
+        x0_rows = keep.tile([P, CH], BF16)
+        nc.vector.memset(x0_rows[:], 0.0)
+
+        x1_sb = keep.tile([P, TOKENS, CH], BF16)
+        bias_sb = keep.tile([P, N_OUT], BF16)
+        w_raw = [keep.tile([P, PACK, 2 * N_TILE], BF16, name="w_raw_%d" % l) for l in range(W_LOADS)]
+        x2_half = [keep.tile([P, HALF_J, CH], BF16, name="x2_half_%d" % x) for x in range(2 * TOKENS)]
+
+        def load_w(l):
+            c, side = divmod(l, 2)
+            cols = slice(side * 2 * N_TILE, (side + 1) * 2 * N_TILE)
+            nc.sync.dma_start(out=w_raw[l][:], in_=w_rows[c][:, :, cols])
+
+        def load_x2(x):
+            r, h = divmod(x, 2)
+            nc.sync.dma_start(out=x2_half[x][:], in_=x2_tokens[:, r, h * HALF_J : (h + 1) * HALF_J, :])
+
+        def hide_diagonal(x):
+            r, h = divmod(x, 2)
+            for i in range(h * HALF_J + r, (h + 1) * HALF_J, TOKENS):
+                neighbour = i + 1 - 2 * r
+                nc.sync.dma_start(
+                    out=x2_half[x][i // TOKENS : P : SAME_SCENE, i - h * HALF_J, :],
+                    in_=x2[:, i, neighbour, :],
+                )
+
+        with tc.manual_schedule():
+            load_w(0)
+            load_x2(0)
+            load_w(1)
+            hide_diagonal(0)
+            nc.sync.dma_start(out=x1_sb[:], in_=x1_tokens)
+            nc.sync.dma_start(out=x0_rows[0:SCENES, :], in_=x0)
+            for x in range(1, 2 * TOKENS):
+                load_x2(x)
+                load_w(x + 1)
+                hide_diagonal(x)
+            load_w(5)
+            nc.sync.dma_start(out=bias_sb[:], in_=b1.partition_broadcast(P))
+            load_w(6)
+            load_w(7)
+
+        w_codes = keep.tile([P, PASSES, N_OUT], U32, align_bytes=64)
+        w_scales = keep.tile([P, PASSES, N_OUT], U8, align_bytes=64)
+        w_grouped = {}
+
+        def regroup_w(w):
+            copy = nc.vector.tensor_copy if w >= W_PIECES - VECTOR_PIECES else nc.scalar.copy
+            cols = slice((w % 2) * N_TILE, (w % 2 + 1) * N_TILE)
+            w_grouped[w] = stage.tile([P, N_TILE, PACK], BF16, name="w_grouped", align_bytes=64)
+            copy(
+                out=w_grouped[w][:].rearrange("p (g i) t -> p g t i", i=4),
+                in_=w_raw[w // 2][:, :, cols].rearrange("p t (g i) -> p g t i", i=4),
+            )
+
+        def quantise_w(w):
+            c, n = divmod(w, N_TILES)
+            cols = slice(n * N_TILE, (n + 1) * N_TILE)
+            nc.vector.quantize_mx(
+                out=w_codes[:, c, cols].bitcast(FP8X4),
+                scales=w_scales[:, c, cols],
+                in_=w_grouped[w][:].rearrange("p n t -> p (n t)"),
+            )
+
+        def reduce_x2(x):
+            r, h = divmod(x, 2)
+            four, two, one = {}, {}, {}
+            for name, op in EXTREMES:
+                four[name] = tree.tile([P, 4, CH], BF16, name="four_" + name)
+                nc.vector.tensor_tensor(
+                    out=four[name][:], in0=x2_half[x][:, 0:4, :], in1=x2_half[x][:, 4:8, :], op=op
+                )
+            for name, op in EXTREMES:
+                two[name] = tree.tile([P, 2, CH], BF16, name="two_" + name)
+                nc.vector.tensor_tensor(
+                    out=two[name][:], in0=four[name][:, 0:2, :], in1=four[name][:, 2:4, :], op=op
+                )
+            for name, op in EXTREMES:
+                one[name] = tree.tile([P, CH], BF16, name="one_" + name)
+                nc.vector.tensor_tensor(
+                    out=one[name][:], in0=two[name][:, 0, :], in1=two[name][:, 1, :], op=op
+                )
+            for name, op in EXTREMES:
+                nc.vector.tensor_tensor(
+                    out=run[name][:, r, :], in0=run[name][:, r, :], in1=one[name][:], op=op
+                )
+
+        f1_codes = keep.tile([P, TOKENS, PASSES, P], U32, align_bytes=64)
+        f1_scales = keep.tile([P, TOKENS, PASSES, P], U8, align_bytes=64)
+        turned = {}
+
+        def turn_f1(r):
+            parts = (x0_rows[:], x1_sb[:, r, :], run["max"][:, r, :], run["min"][:, r, :])
+            for c in range(PASSES):
+                if c % 2 == 0:
+                    bank = psum.tile(
+                        [P, 2, 2, P], F32, tag="bank%d" % (N_TILES + 2 * r + c // 2), name="turned"
+                    )
+                turned[c] = bank[:, c % 2, :, :]
+                words = parts[c].bitcast(F32)
+                for u in range(2):
+                    nc.tensor.transpose(turned[c][:, u, :], words[:, u : CH // 2 : 2], ident[:])
+
+        def quantise_f1(r):
+            grouped = keep.tile([P, PASSES, P, PACK], BF16, name="f1_grouped_%d" % r, align_bytes=64)
+            words = grouped[:].bitcast(F32)
+            nc.vector.tensor_copy(
+                out=words[:, 0, :, :].rearrange("p (b g) u -> p b g u", g=SAME_SCENE),
+                in_=turned[0][:, :, 0:SCENES]
+                .rearrange("p u b -> p b u")
+                .unsqueeze(2)
+                .to_broadcast([P, SCENES, SAME_SCENE, 2]),
+            )
+            for c in range(1, PASSES):
+                nc.vector.tensor_copy(out=words[:, c, :, :], in_=turned[c].rearrange("p u m -> p m u"))
+            nc.vector.quantize_mx(
+                out=f1_codes[:, r, :, :].rearrange("p c m -> p (c m)").bitcast(FP8X4),
+                scales=f1_scales[:, r, :, :].rearrange("p c m -> p (c m)"),
+                in_=grouped[:].rearrange("p c m t -> p (c m t)"),
+            )
+
+        sums = {}
+
+        def multiply(r, w):
+            c, n = divmod(w, N_TILES)
+            cols = slice(n * N_TILE, (n + 1) * N_TILE)
+            if c == 0:
+                sums[(r, n)] = psum.tile([P, N_TILE], F32, tag="bank%d" % (r * N_TILES + n), name="sums")
+            nc.tensor.matmul_mx(
+                out=sums[(r, n)][:],
+                lhsT=f1_codes[:, r, c, :].bitcast(FP8X4),
+                lhsT_scale=f1_scales[:, r, c, :],
+                rhs=w_codes[:, c, cols].bitcast(FP8X4),
+                rhs_scale=w_scales[:, c, cols],
+                start=(c == 0),
+                stop=(c == PASSES - 1),
+            )
+
+        def finish(n):
+            cols = slice(n * N_TILE, (n + 1) * N_TILE)
+            result = results.tile([P, TOKENS, N_TILE], F32)
+            for r in range(TOKENS):
+                nc.vector.tensor_tensor(
+                    out=result[:, r, :], in0=sums[(r, n)][:], in1=bias_sb[:, cols], op=ALU.add
+                )
+                nc.scalar.activation(out=result[:, r, :], in_=result[:, r, :], func=ACT.Sigmoid)
+            nc.sync.dma_start(out=out_tokens[:, :, cols], in_=result[:])
+
+        complete = []
+        for l in range(W_LOADS + 1):
+            if l < W_LOADS:
+                regroup_w(2 * l)
+                regroup_w(2 * l + 1)
+            x = l - 1
+            last_half_of_token = 0 <= x < 2 * TOKENS and x % 2 == 1
+            if 0 <= x < 2 * TOKENS:
+                reduce_x2(x)
+            if last_half_of_token:
+                turn_f1(x // 2)
+            if l >= 1:
+                for w in (2 * l - 2, 2 * l - 1):
+                    quantise_w(w)
+                    for r in complete:
+                        multiply(r, w)
+                for w in (2 * l - 2, 2 * l - 1):
+                    if w // N_TILES == PASSES - 1:
+                        finish(w % N_TILES)
+            if last_half_of_token:
+                quantise_f1(x // 2)
+                for w in range(2 * l):
+                    multiply(x // 2, w)
+                complete.append(x // 2)

@@ -25,7 +25,8 @@ SAME_SCENE = P // SCENES
 HALF_J = OBJECTS // 2
 W_PIECES = PASSES * N_TILES
 W_LOADS = W_PIECES // 2
-VECTOR_PIECES = 2
+X2_LOADS = 2 * TOKENS
+VECTOR_LOADS = 2
 EXTREMES = (("max", ALU.max), ("min", ALU.min))
 
 FLOPS = 2 * SCENES * OBJECTS * PASSES * CH * N_OUT
@@ -39,10 +40,11 @@ def tile_differentiablelogicmachine_pb_kernel(tc, x0, x1, x2, W1, b1, out):
     w_rows = W1.rearrange("(c p t) n -> c p t n", p=P, t=PACK)
 
     with ExitStack() as ctx:
+        ctx.enter_context(tc.manual_schedule())
         keep = ctx.enter_context(tc.tile_pool(name="keep", bufs=1))
         stage = ctx.enter_context(tc.tile_pool(name="stage", bufs=6))
-        tree = ctx.enter_context(tc.tile_pool(name="tree", bufs=2))
-        results = ctx.enter_context(tc.tile_pool(name="results", bufs=3))
+        tree = ctx.enter_context(tc.tile_pool(name="tree", bufs=1))
+        results = ctx.enter_context(tc.tile_pool(name="results", bufs=N_TILES))
         psum = ctx.enter_context(tc.psum_pool(name="psum", bufs=1))
 
         ident = keep.tile([P, P], F32)
@@ -60,7 +62,7 @@ def tile_differentiablelogicmachine_pb_kernel(tc, x0, x1, x2, W1, b1, out):
         x1_sb = keep.tile([P, TOKENS, CH], BF16)
         bias_sb = keep.tile([P, N_OUT], BF16)
         w_raw = [keep.tile([P, PACK, 2 * N_TILE], BF16, name="w_raw_%d" % l) for l in range(W_LOADS)]
-        x2_half = [keep.tile([P, HALF_J, CH], BF16, name="x2_half_%d" % x) for x in range(2 * TOKENS)]
+        x2_half = [keep.tile([P, HALF_J, CH], BF16, name="x2_half_%d" % x) for x in range(X2_LOADS)]
 
         def load_w(l):
             c, side = divmod(l, 2)
@@ -80,28 +82,25 @@ def tile_differentiablelogicmachine_pb_kernel(tc, x0, x1, x2, W1, b1, out):
                     in_=x2[:, i, neighbour, :],
                 )
 
-        with tc.manual_schedule():
-            load_w(0)
-            load_x2(0)
-            load_w(1)
-            hide_diagonal(0)
-            nc.sync.dma_start(out=x1_sb[:], in_=x1_tokens)
-            nc.sync.dma_start(out=x0_rows[0:SCENES, :], in_=x0)
-            for x in range(1, 2 * TOKENS):
-                load_x2(x)
-                load_w(x + 1)
-                hide_diagonal(x)
-            load_w(5)
-            nc.sync.dma_start(out=bias_sb[:], in_=b1.partition_broadcast(P))
-            load_w(6)
-            load_w(7)
+        for x in range(X2_LOADS):
+            load_x2(x)
+            load_w(x)
+            hide_diagonal(x)
+            if x == 1:
+                nc.sync.dma_start(out=x1_sb[:], in_=x1_tokens)
+                nc.sync.dma_start(out=x0_rows[0:SCENES, :], in_=x0)
+        for l in range(X2_LOADS, W_LOADS):
+            load_w(l)
+            if l == W_LOADS - 3:
+                nc.sync.dma_start(out=bias_sb[:], in_=b1.partition_broadcast(P))
 
         w_codes = keep.tile([P, PASSES, N_OUT], U32, align_bytes=64)
         w_scales = keep.tile([P, PASSES, N_OUT], U8, align_bytes=64)
         w_grouped = {}
 
         def regroup_w(w):
-            copy = nc.vector.tensor_copy if w >= W_PIECES - VECTOR_PIECES else nc.scalar.copy
+            by_vector = w % 2 == 1 and w // 2 >= W_LOADS - VECTOR_LOADS
+            copy = nc.vector.tensor_copy if by_vector else nc.scalar.copy
             cols = slice((w % 2) * N_TILE, (w % 2 + 1) * N_TILE)
             w_grouped[w] = stage.tile([P, N_TILE, PACK], BF16, name="w_grouped", align_bytes=64)
             copy(
@@ -157,9 +156,11 @@ def tile_differentiablelogicmachine_pb_kernel(tc, x0, x1, x2, W1, b1, out):
                 for u in range(2):
                     nc.tensor.transpose(turned[c][:, u, :], words[:, u : CH // 2 : 2], ident[:])
 
-        def quantise_f1(r):
-            grouped = keep.tile([P, PASSES, P, PACK], BF16, name="f1_grouped_%d" % r, align_bytes=64)
-            words = grouped[:].bitcast(F32)
+        f1_grouped = {}
+
+        def pack_f1(r):
+            f1_grouped[r] = keep.tile([P, PASSES, P, PACK], BF16, name="f1_grouped_%d" % r, align_bytes=64)
+            words = f1_grouped[r][:].bitcast(F32)
             nc.vector.tensor_copy(
                 out=words[:, 0, :, :].rearrange("p (b g) u -> p b g u", g=SAME_SCENE),
                 in_=turned[0][:, :, 0:SCENES]
@@ -169,10 +170,12 @@ def tile_differentiablelogicmachine_pb_kernel(tc, x0, x1, x2, W1, b1, out):
             )
             for c in range(1, PASSES):
                 nc.vector.tensor_copy(out=words[:, c, :, :], in_=turned[c].rearrange("p u m -> p m u"))
+
+        def quantise_f1(r):
             nc.vector.quantize_mx(
                 out=f1_codes[:, r, :, :].rearrange("p c m -> p (c m)").bitcast(FP8X4),
                 scales=f1_scales[:, r, :, :].rearrange("p c m -> p (c m)"),
-                in_=grouped[:].rearrange("p c m t -> p (c m t)"),
+                in_=f1_grouped[r][:].rearrange("p c m t -> p (c m t)"),
             )
 
         sums = {}
@@ -200,29 +203,31 @@ def tile_differentiablelogicmachine_pb_kernel(tc, x0, x1, x2, W1, b1, out):
                     out=result[:, r, :], in0=sums[(r, n)][:], in1=bias_sb[:, cols], op=ALU.add
                 )
                 nc.scalar.activation(out=result[:, r, :], in_=result[:, r, :], func=ACT.Sigmoid)
-            nc.sync.dma_start(out=out_tokens[:, :, cols], in_=result[:])
+                nc.sync.dma_start(out=out_tokens[:, r, cols], in_=result[:, r, :])
 
         complete = []
         for l in range(W_LOADS + 1):
+            token = l // 2 - 1 if l % 2 == 0 and 2 <= l <= X2_LOADS else None
             if l < W_LOADS:
                 regroup_w(2 * l)
                 regroup_w(2 * l + 1)
-            x = l - 1
-            last_half_of_token = 0 <= x < 2 * TOKENS and x % 2 == 1
-            if 0 <= x < 2 * TOKENS:
-                reduce_x2(x)
-            if last_half_of_token:
-                turn_f1(x // 2)
             if l >= 1:
                 for w in (2 * l - 2, 2 * l - 1):
                     quantise_w(w)
                     for r in complete:
                         multiply(r, w)
+            if token is not None:
+                pack_f1(token)
+            if l >= 1:
                 for w in (2 * l - 2, 2 * l - 1):
                     if w // N_TILES == PASSES - 1:
                         finish(w % N_TILES)
-            if last_half_of_token:
-                quantise_f1(x // 2)
+            if l < X2_LOADS:
+                reduce_x2(l)
+                if l % 2 == 1:
+                    turn_f1(l // 2)
+            if token is not None:
+                quantise_f1(token)
                 for w in range(2 * l):
-                    multiply(x // 2, w)
-                complete.append(x // 2)
+                    multiply(token, w)
+                complete.append(token)

@@ -26,7 +26,7 @@ HALF_J = OBJECTS // 2
 W_PIECES = PASSES * N_TILES
 W_LOADS = W_PIECES // 2
 X2_LOADS = 2 * TOKENS
-VECTOR_LOADS = 2
+VECTOR_LOADS = 3
 EXTREMES = (("max", ALU.max), ("min", ALU.min))
 
 FLOPS = 2 * SCENES * OBJECTS * PASSES * CH * N_OUT
@@ -49,6 +49,8 @@ def tile_differentiablelogicmachine_pb_kernel(tc, x0, x1, x2, W1, b1, out):
 
         ident = keep.tile([P, P], F32)
         make_identity(nc, ident[:])
+        x0_rows = keep.tile([P, CH], BF16)
+        nc.vector.memset(x0_rows[:], 0.0)
         warm = keep.tile([P, 1], F32)
         nc.vector.memset(warm[:], 0.0)
         nc.scalar.activation(out=warm[:], in_=warm[:], func=ACT.Sigmoid)
@@ -56,8 +58,6 @@ def tile_differentiablelogicmachine_pb_kernel(tc, x0, x1, x2, W1, b1, out):
         for name, fill in (("max", 0.0), ("min", 1.0)):
             run[name] = keep.tile([P, TOKENS, CH], BF16, name="run_" + name)
             nc.vector.memset(run[name][:], fill)
-        x0_rows = keep.tile([P, CH], BF16)
-        nc.vector.memset(x0_rows[:], 0.0)
 
         x1_sb = keep.tile([P, TOKENS, CH], BF16)
         bias_sb = keep.tile([P, N_OUT], BF16)
@@ -84,11 +84,11 @@ def tile_differentiablelogicmachine_pb_kernel(tc, x0, x1, x2, W1, b1, out):
 
         for x in range(X2_LOADS):
             load_x2(x)
-            load_w(x)
-            hide_diagonal(x)
-            if x == 1:
+            if x == 0:
                 nc.sync.dma_start(out=x1_sb[:], in_=x1_tokens)
                 nc.sync.dma_start(out=x0_rows[0:SCENES, :], in_=x0)
+            load_w(x)
+            hide_diagonal(x)
         for l in range(X2_LOADS, W_LOADS):
             load_w(l)
             if l == W_LOADS - 3:
@@ -142,40 +142,40 @@ def tile_differentiablelogicmachine_pb_kernel(tc, x0, x1, x2, W1, b1, out):
 
         f1_codes = keep.tile([P, TOKENS, PASSES, P], U32, align_bytes=64)
         f1_scales = keep.tile([P, TOKENS, PASSES, P], U8, align_bytes=64)
+        f1_grouped = [
+            keep.tile([P, PASSES, P, PACK], BF16, name="f1_grouped_%d" % r, align_bytes=64) for r in range(TOKENS)
+        ]
         turned = {}
 
-        def turn_f1(r):
-            parts = (x0_rows[:], x1_sb[:, r, :], run["max"][:, r, :], run["min"][:, r, :])
-            for c in range(PASSES):
-                if c % 2 == 0:
-                    bank = psum.tile(
-                        [P, 2, 2, P], F32, tag="bank%d" % (N_TILES + 2 * r + c // 2), name="turned"
-                    )
-                turned[c] = bank[:, c % 2, :, :]
-                words = parts[c].bitcast(F32)
+        def turn_f1(r, part):
+            sources = (x0_rows[:], x1_sb[:, r, :], run["max"][:, r, :], run["min"][:, r, :])
+            bank = psum.tile([P, 2, 2, P], F32, tag="bank%d" % (N_TILES + 2 * r + part), name="turned")
+            for c in (2 * part, 2 * part + 1):
+                turned[(r, c)] = bank[:, c % 2, :, :]
+                words = sources[c].bitcast(F32)
                 for u in range(2):
-                    nc.tensor.transpose(turned[c][:, u, :], words[:, u : CH // 2 : 2], ident[:])
+                    nc.tensor.transpose(turned[(r, c)][:, u, :], words[:, u : CH // 2 : 2], ident[:])
 
-        f1_grouped = {}
-
-        def pack_f1(r):
-            f1_grouped[r] = keep.tile([P, PASSES, P, PACK], BF16, name="f1_grouped_%d" % r, align_bytes=64)
+        def pack_f1(r, part):
             words = f1_grouped[r][:].bitcast(F32)
-            nc.vector.tensor_copy(
-                out=words[:, 0, :, :].rearrange("p (b g) u -> p b g u", g=SAME_SCENE),
-                in_=turned[0][:, :, 0:SCENES]
-                .rearrange("p u b -> p b u")
-                .unsqueeze(2)
-                .to_broadcast([P, SCENES, SAME_SCENE, 2]),
-            )
-            for c in range(1, PASSES):
-                nc.vector.tensor_copy(out=words[:, c, :, :], in_=turned[c].rearrange("p u m -> p m u"))
+            for c in (2 * part, 2 * part + 1):
+                if c == 0:
+                    nc.scalar.copy(
+                        out=words[:, c, :, :].rearrange("p (b g) u -> p b g u", g=SAME_SCENE),
+                        in_=turned[(r, c)][:, :, 0:SCENES]
+                        .rearrange("p u b -> p b u")
+                        .unsqueeze(2)
+                        .to_broadcast([P, SCENES, SAME_SCENE, 2]),
+                    )
+                else:
+                    nc.scalar.copy(out=words[:, c, :, :], in_=turned[(r, c)].rearrange("p u m -> p m u"))
 
-        def quantise_f1(r):
+        def quantise_f1(r, part):
+            passes = slice(2 * part, 2 * part + 2)
             nc.vector.quantize_mx(
-                out=f1_codes[:, r, :, :].rearrange("p c m -> p (c m)").bitcast(FP8X4),
-                scales=f1_scales[:, r, :, :].rearrange("p c m -> p (c m)"),
-                in_=f1_grouped[r][:].rearrange("p c m t -> p (c m t)"),
+                out=f1_codes[:, r, passes, :].rearrange("p c m -> p (c m)").bitcast(FP8X4),
+                scales=f1_scales[:, r, passes, :].rearrange("p c m -> p (c m)"),
+                in_=f1_grouped[r][:, passes, :, :].rearrange("p c m t -> p (c m t)"),
             )
 
         sums = {}
@@ -205,29 +205,37 @@ def tile_differentiablelogicmachine_pb_kernel(tc, x0, x1, x2, W1, b1, out):
                 nc.scalar.activation(out=result[:, r, :], in_=result[:, r, :], func=ACT.Sigmoid)
                 nc.sync.dma_start(out=out_tokens[:, r, cols], in_=result[:, r, :])
 
-        complete = []
+        for r in range(TOKENS):
+            turn_f1(r, 0)
+        for r in range(TOKENS):
+            pack_f1(r, 0)
+        for r in range(TOKENS):
+            quantise_f1(r, 0)
+        multiplying = [0]
         for l in range(W_LOADS + 1):
-            token = l // 2 - 1 if l % 2 == 0 and 2 <= l <= X2_LOADS else None
+            done = (2 * l - 2, 2 * l - 1) if l >= 1 else ()
             if l < W_LOADS:
                 regroup_w(2 * l)
                 regroup_w(2 * l + 1)
-            if l >= 1:
-                for w in (2 * l - 2, 2 * l - 1):
-                    quantise_w(w)
-                    for r in complete:
-                        multiply(r, w)
-            if token is not None:
-                pack_f1(token)
-            if l >= 1:
-                for w in (2 * l - 2, 2 * l - 1):
-                    if w // N_TILES == PASSES - 1:
-                        finish(w % N_TILES)
+            for r in range(TOKENS):
+                if l == 2 * r + 2:
+                    pack_f1(r, 1)
+            for w in done:
+                quantise_w(w)
+            for r in range(TOKENS):
+                if l == 2 * r + 3:
+                    quantise_f1(r, 1)
+                    if r not in multiplying:
+                        for w in range(done[0]):
+                            multiply(r, w)
+                        multiplying.append(r)
+            for w in done:
+                for r in multiplying:
+                    multiply(r, w)
+            for w in done:
+                if w // N_TILES == PASSES - 1:
+                    finish(w % N_TILES)
             if l < X2_LOADS:
                 reduce_x2(l)
                 if l % 2 == 1:
-                    turn_f1(l // 2)
-            if token is not None:
-                quantise_f1(token)
-                for w in range(2 * l):
-                    multiply(token, w)
-                complete.append(token)
+                    turn_f1(l // 2, 1)

@@ -26,6 +26,7 @@ HALF_J = OBJECTS // 2
 W_PIECES = PASSES * N_TILES
 W_LOADS = W_PIECES // 2
 X2_LOADS = 2 * TOKENS
+TENSOR_PIECES = (1, 3, 5)
 VECTOR_LOADS = 3
 EXTREMES = (("max", ALU.max), ("min", ALU.min))
 
@@ -49,6 +50,8 @@ def tile_differentiablelogicmachine_pb_kernel(tc, x0, x1, x2, W1, b1, out):
 
         ident = keep.tile([P, P], F32)
         make_identity(nc, ident[:])
+        ident_bf = keep.tile([P, P], BF16)
+        make_identity(nc, ident_bf[:])
         x0_rows = keep.tile([P, CH], BF16)
         nc.vector.memset(x0_rows[:], 0.0)
         warm = keep.tile([P, 1], F32)
@@ -97,6 +100,23 @@ def tile_differentiablelogicmachine_pb_kernel(tc, x0, x1, x2, W1, b1, out):
         w_codes = keep.tile([P, PASSES, N_OUT], U32, align_bytes=64)
         w_scales = keep.tile([P, PASSES, N_OUT], U8, align_bytes=64)
         w_grouped = {}
+
+        def move_w(w):
+            half = N_TILE // 2
+            w_grouped[w] = stage.tile([P, N_TILE, PACK], BF16, name="w_grouped", align_bytes=64)
+            for side in range(2):
+                moved = psum.tile([P, half, PACK], BF16, tag="bank%d" % (N_TILES + 2 * side), name="moved")
+                for q in range(2):
+                    cols = slice(q * half // 2, (q + 1) * half // 2)
+                    at = (w % 2) * N_TILE + side * half + q * half // 2
+                    nc.tensor.matmul(
+                        out=moved[:, cols, :],
+                        lhsT=ident_bf[:],
+                        rhs=w_raw[w // 2][:, :, at : at + half // 2].rearrange("p t n -> p n t"),
+                        start=True,
+                        stop=True,
+                    )
+                nc.scalar.copy(out=w_grouped[w][:, side * half : (side + 1) * half, :], in_=moved[:])
 
         def regroup_w(w):
             by_vector = w % 2 == 1 and w // 2 >= W_LOADS - VECTOR_LOADS
@@ -215,8 +235,11 @@ def tile_differentiablelogicmachine_pb_kernel(tc, x0, x1, x2, W1, b1, out):
         for l in range(W_LOADS + 1):
             done = (2 * l - 2, 2 * l - 1) if l >= 1 else ()
             if l < W_LOADS:
-                regroup_w(2 * l)
-                regroup_w(2 * l + 1)
+                for w in (2 * l, 2 * l + 1):
+                    if w in TENSOR_PIECES:
+                        move_w(w)
+                    else:
+                        regroup_w(w)
             for r in range(TOKENS):
                 if l == 2 * r + 2:
                     pack_f1(r, 1)

@@ -22,13 +22,13 @@ N_TILE = 512
 N_TILES = N_OUT // N_TILE
 TOKENS = 2
 SAME_SCENE = P // SCENES
-HALF_J = OBJECTS // 2
-W_PIECES = PASSES * N_TILES
-W_LOADS = W_PIECES // 2
-X2_LOADS = 2 * TOKENS
-TENSOR_PIECES = (1, 3, 5)
-VECTOR_LOADS = 3
-EXTREMES = (("max", ALU.max), ("min", ALU.min))
+HALF = OBJECTS // 2
+X2_UNITS = tuple((r, h * HALF, HALF) for r in range(TOKENS) for h in range(2))
+PIECES = PASSES * N_TILES
+SINGLE = 2
+TENSOR_PIECES = (3, 5, 7)
+VECTOR_PIECES = (9, 11, 13, 15)
+EXTREMES = (("max", ALU.max, 0.0), ("min", ALU.min, 1.0))
 
 FLOPS = 2 * SCENES * OBJECTS * PASSES * CH * N_OUT
 
@@ -43,9 +43,9 @@ def tile_differentiablelogicmachine_pb_kernel(tc, x0, x1, x2, W1, b1, out):
     with ExitStack() as ctx:
         ctx.enter_context(tc.manual_schedule())
         keep = ctx.enter_context(tc.tile_pool(name="keep", bufs=1))
-        stage = ctx.enter_context(tc.tile_pool(name="stage", bufs=6))
+        stage = ctx.enter_context(tc.tile_pool(name="stage", bufs=8))
         tree = ctx.enter_context(tc.tile_pool(name="tree", bufs=1))
-        results = ctx.enter_context(tc.tile_pool(name="results", bufs=N_TILES))
+        results = ctx.enter_context(tc.tile_pool(name="results", bufs=8))
         psum = ctx.enter_context(tc.psum_pool(name="psum", bufs=1))
 
         ident = keep.tile([P, P], F32)
@@ -57,79 +57,91 @@ def tile_differentiablelogicmachine_pb_kernel(tc, x0, x1, x2, W1, b1, out):
         warm = keep.tile([P, 1], F32)
         nc.vector.memset(warm[:], 0.0)
         nc.scalar.activation(out=warm[:], in_=warm[:], func=ACT.Sigmoid)
-        run = {}
-        for name, fill in (("max", 0.0), ("min", 1.0)):
-            run[name] = keep.tile([P, TOKENS, CH], BF16, name="run_" + name)
-            nc.vector.memset(run[name][:], fill)
 
         x1_sb = keep.tile([P, TOKENS, CH], BF16)
         bias_sb = keep.tile([P, N_OUT], BF16)
-        w_raw = [keep.tile([P, PACK, 2 * N_TILE], BF16, name="w_raw_%d" % l) for l in range(W_LOADS)]
-        x2_half = [keep.tile([P, HALF_J, CH], BF16, name="x2_half_%d" % x) for x in range(X2_LOADS)]
+        w_raw = {}
 
-        def load_w(l):
-            c, side = divmod(l, 2)
-            cols = slice(side * 2 * N_TILE, (side + 1) * 2 * N_TILE)
-            nc.sync.dma_start(out=w_raw[l][:], in_=w_rows[c][:, :, cols])
+        def piece(w):
+            return divmod(w, N_TILES)
+
+        def load_w(w, count):
+            c, n = piece(w)
+            raw = keep.tile([P, PACK, count * N_TILE], BF16, name="w_raw_%d" % w)
+            nc.sync.dma_start(out=raw[:], in_=w_rows[c][:, :, n * N_TILE : (n + count) * N_TILE])
+            for i in range(count):
+                w_raw[w + i] = raw[:, :, i * N_TILE : (i + 1) * N_TILE]
+
+        x2_sb = [keep.tile([P, n, CH], BF16, name="x2_%d" % x) for x, (r, j, n) in enumerate(X2_UNITS)]
 
         def load_x2(x):
-            r, h = divmod(x, 2)
-            nc.sync.dma_start(out=x2_half[x][:], in_=x2_tokens[:, r, h * HALF_J : (h + 1) * HALF_J, :])
+            r, j, n = X2_UNITS[x]
+            nc.sync.dma_start(out=x2_sb[x][:], in_=x2_tokens[:, r, j : j + n, :])
 
         def hide_diagonal(x):
-            r, h = divmod(x, 2)
-            for i in range(h * HALF_J + r, (h + 1) * HALF_J, TOKENS):
+            r, j, n = X2_UNITS[x]
+            for i in range(j + r, j + n, TOKENS):
                 neighbour = i + 1 - 2 * r
                 nc.sync.dma_start(
-                    out=x2_half[x][i // TOKENS : P : SAME_SCENE, i - h * HALF_J, :],
+                    out=x2_sb[x][i // TOKENS : P : SAME_SCENE, i - j, :],
                     in_=x2[:, i, neighbour, :],
                 )
 
-        for x in range(X2_LOADS):
-            load_x2(x)
-            if x == 0:
-                nc.sync.dma_start(out=x1_sb[:], in_=x1_tokens)
-                nc.sync.dma_start(out=x0_rows[0:SCENES, :], in_=x0)
-            load_w(x)
-            hide_diagonal(x)
-        for l in range(X2_LOADS, W_LOADS):
-            load_w(l)
-            if l == W_LOADS - 3:
-                nc.sync.dma_start(out=bias_sb[:], in_=b1.partition_broadcast(P))
+        load_x2(0)
+        load_w(0, 1)
+        load_w(1, 1)
+        hide_diagonal(0)
+        load_x2(1)
+        nc.sync.dma_start(out=x1_sb[:], in_=x1_tokens)
+        nc.sync.dma_start(out=x0_rows[0:SCENES, :], in_=x0)
+        load_w(2, 2)
+        hide_diagonal(1)
+        load_x2(2)
+        load_w(4, 2)
+        hide_diagonal(2)
+        load_x2(3)
+        load_w(6, 2)
+        hide_diagonal(3)
+        load_w(8, 4)
+        load_w(12, 4)
+        nc.sync.dma_start(out=bias_sb[:], in_=b1.partition_broadcast(P))
 
         w_codes = keep.tile([P, PASSES, N_OUT], U32, align_bytes=64)
         w_scales = keep.tile([P, PASSES, N_OUT], U8, align_bytes=64)
         w_grouped = {}
 
+        moved = {}
+
         def move_w(w):
             half = N_TILE // 2
-            w_grouped[w] = stage.tile([P, N_TILE, PACK], BF16, name="w_grouped", align_bytes=64)
             for side in range(2):
-                moved = psum.tile([P, half, PACK], BF16, tag="bank%d" % (N_TILES + 2 * side), name="moved")
+                moved[(w, side)] = psum.tile([P, half, PACK], BF16, tag="bank%d" % (4 + side), name="moved")
                 for q in range(2):
                     cols = slice(q * half // 2, (q + 1) * half // 2)
-                    at = (w % 2) * N_TILE + side * half + q * half // 2
+                    at = side * half + q * half // 2
                     nc.tensor.matmul(
-                        out=moved[:, cols, :],
+                        out=moved[(w, side)][:, cols, :],
                         lhsT=ident_bf[:],
-                        rhs=w_raw[w // 2][:, :, at : at + half // 2].rearrange("p t n -> p n t"),
+                        rhs=w_raw[w][:, :, at : at + half // 2].rearrange("p t n -> p n t"),
                         start=True,
                         stop=True,
                     )
-                nc.scalar.copy(out=w_grouped[w][:, side * half : (side + 1) * half, :], in_=moved[:])
 
         def regroup_w(w):
-            by_vector = w % 2 == 1 and w // 2 >= W_LOADS - VECTOR_LOADS
-            copy = nc.vector.tensor_copy if by_vector else nc.scalar.copy
-            cols = slice((w % 2) * N_TILE, (w % 2 + 1) * N_TILE)
             w_grouped[w] = stage.tile([P, N_TILE, PACK], BF16, name="w_grouped", align_bytes=64)
+            if w in TENSOR_PIECES:
+                for side in range(2):
+                    half = N_TILE // 2
+                    nc.scalar.copy(out=w_grouped[w][:, side * half : (side + 1) * half, :], in_=moved[(w, side)][:])
+                return
+            copy = nc.vector.tensor_copy if w in VECTOR_PIECES else nc.scalar.copy
             copy(
                 out=w_grouped[w][:].rearrange("p (g i) t -> p g t i", i=4),
-                in_=w_raw[w // 2][:, :, cols].rearrange("p t (g i) -> p g t i", i=4),
+                in_=w_raw[w].rearrange("p t (g i) -> p g t i", i=4),
             )
 
         def quantise_w(w):
-            c, n = divmod(w, N_TILES)
+            c, n = piece(w)
             cols = slice(n * N_TILE, (n + 1) * N_TILE)
             nc.vector.quantize_mx(
                 out=w_codes[:, c, cols].bitcast(FP8X4),
@@ -137,28 +149,44 @@ def tile_differentiablelogicmachine_pb_kernel(tc, x0, x1, x2, W1, b1, out):
                 in_=w_grouped[w][:].rearrange("p n t -> p (n t)"),
             )
 
-        def reduce_x2(x):
-            r, h = divmod(x, 2)
-            four, two, one = {}, {}, {}
-            for name, op in EXTREMES:
-                four[name] = tree.tile([P, 4, CH], BF16, name="four_" + name)
-                nc.vector.tensor_tensor(
-                    out=four[name][:], in0=x2_half[x][:, 0:4, :], in1=x2_half[x][:, 4:8, :], op=op
-                )
-            for name, op in EXTREMES:
-                two[name] = tree.tile([P, 2, CH], BF16, name="two_" + name)
-                nc.vector.tensor_tensor(
-                    out=two[name][:], in0=four[name][:, 0:2, :], in1=four[name][:, 2:4, :], op=op
-                )
-            for name, op in EXTREMES:
-                one[name] = tree.tile([P, CH], BF16, name="one_" + name)
-                nc.vector.tensor_tensor(
-                    out=one[name][:], in0=two[name][:, 0, :], in1=two[name][:, 1, :], op=op
-                )
-            for name, op in EXTREMES:
-                nc.vector.tensor_tensor(
-                    out=run[name][:, r, :], in0=run[name][:, r, :], in1=one[name][:], op=op
-                )
+        run = {name: keep.tile([P, TOKENS, CH], BF16, name="run_" + name) for name, op, fill in EXTREMES}
+
+        first_level = {}
+
+        def reduce_clean(x):
+            r, j, n = X2_UNITS[x]
+            for name, op, fill in EXTREMES:
+                level = tree.tile([P, 2, n // 4, CH], BF16, name="level_" + name)
+                first_level[(x, name)] = level
+                clean = x2_sb[x][:].rearrange("p (h k t) c -> p t h k c", h=2, t=TOKENS)[:, 1 - r]
+                nc.vector.tensor_tensor(out=level[:, 0], in0=clean[:, 0], in1=clean[:, 1], op=op)
+
+        def reduce_rest(x):
+            r, j, n = X2_UNITS[x]
+            parts = {}
+            for name, op, fill in EXTREMES:
+                level = first_level[(x, name)]
+                rest = x2_sb[x][:].rearrange("p (h k t) c -> p t h k c", h=2, t=TOKENS)[:, r]
+                nc.vector.tensor_tensor(out=level[:, 1], in0=rest[:, 0], in1=rest[:, 1], op=op)
+                parts[name] = level[:].rearrange("p u k c -> p (u k) c")
+            n //= 2
+            while n > 1:
+                n //= 2
+                for name, op, fill in EXTREMES:
+                    level = tree.tile([P, n, CH], BF16, name="down_%d_%s" % (n, name))
+                    nc.vector.tensor_tensor(
+                        out=level[:], in0=parts[name][:, 0:n, :], in1=parts[name][:, n : 2 * n, :], op=op
+                    )
+                    parts[name] = level[:]
+            for name, op, fill in EXTREMES:
+                if j == 0:
+                    nc.vector.tensor_scalar(
+                        out=run[name][:, r, :], in0=parts[name][:, 0, :], scalar1=fill, scalar2=None, op0=op
+                    )
+                else:
+                    nc.vector.tensor_tensor(
+                        out=run[name][:, r, :], in0=run[name][:, r, :], in1=parts[name][:, 0, :], op=op
+                    )
 
         f1_codes = keep.tile([P, TOKENS, PASSES, P], U32, align_bytes=64)
         f1_scales = keep.tile([P, TOKENS, PASSES, P], U8, align_bytes=64)
@@ -167,10 +195,13 @@ def tile_differentiablelogicmachine_pb_kernel(tc, x0, x1, x2, W1, b1, out):
         ]
         turned = {}
 
+        def passes_of(r, part):
+            return (1,) if (r, part) == (1, 0) else (2 * part, 2 * part + 1)
+
         def turn_f1(r, part):
             sources = (x0_rows[:], x1_sb[:, r, :], run["max"][:, r, :], run["min"][:, r, :])
-            bank = psum.tile([P, 2, 2, P], F32, tag="bank%d" % (N_TILES + 2 * r + part), name="turned")
-            for c in (2 * part, 2 * part + 1):
+            bank = psum.tile([P, 2, 2, P], F32, tag="bank%d" % (N_TILES + 2 * part + r), name="turned")
+            for c in passes_of(r, part):
                 turned[(r, c)] = bank[:, c % 2, :, :]
                 words = sources[c].bitcast(F32)
                 for u in range(2):
@@ -178,7 +209,7 @@ def tile_differentiablelogicmachine_pb_kernel(tc, x0, x1, x2, W1, b1, out):
 
         def pack_f1(r, part):
             words = f1_grouped[r][:].bitcast(F32)
-            for c in (2 * part, 2 * part + 1):
+            for c in passes_of(r, part):
                 if c == 0:
                     nc.scalar.copy(
                         out=words[:, c, :, :].rearrange("p (b g) u -> p b g u", g=SAME_SCENE),
@@ -191,7 +222,8 @@ def tile_differentiablelogicmachine_pb_kernel(tc, x0, x1, x2, W1, b1, out):
                     nc.scalar.copy(out=words[:, c, :, :], in_=turned[(r, c)].rearrange("p u m -> p m u"))
 
         def quantise_f1(r, part):
-            passes = slice(2 * part, 2 * part + 2)
+            c = passes_of(r, part)
+            passes = slice(c[0], c[-1] + 1)
             nc.vector.quantize_mx(
                 out=f1_codes[:, r, passes, :].rearrange("p c m -> p (c m)").bitcast(FP8X4),
                 scales=f1_scales[:, r, passes, :].rearrange("p c m -> p (c m)"),
@@ -201,64 +233,110 @@ def tile_differentiablelogicmachine_pb_kernel(tc, x0, x1, x2, W1, b1, out):
         sums = {}
 
         def multiply(r, w):
-            c, n = divmod(w, N_TILES)
+            c, n = piece(w)
             cols = slice(n * N_TILE, (n + 1) * N_TILE)
             if c == 0:
-                sums[(r, n)] = psum.tile([P, N_TILE], F32, tag="bank%d" % (r * N_TILES + n), name="sums")
+                sums[(r, n)] = psum.tile([P, N_TILE], F32, tag="bank%d" % (4 * r + n), name="sums")
+            token = 0 if c == 0 else r
             nc.tensor.matmul_mx(
                 out=sums[(r, n)][:],
-                lhsT=f1_codes[:, r, c, :].bitcast(FP8X4),
-                lhsT_scale=f1_scales[:, r, c, :],
+                lhsT=f1_codes[:, token, c, :].bitcast(FP8X4),
+                lhsT_scale=f1_scales[:, token, c, :],
                 rhs=w_codes[:, c, cols].bitcast(FP8X4),
                 rhs_scale=w_scales[:, c, cols],
                 start=(c == 0),
                 stop=(c == PASSES - 1),
             )
 
+        sigmoids = []
+        finished = []
+
         def finish(n):
             cols = slice(n * N_TILE, (n + 1) * N_TILE)
-            result = results.tile([P, TOKENS, N_TILE], F32)
             for r in range(TOKENS):
-                nc.vector.tensor_tensor(
-                    out=result[:, r, :], in0=sums[(r, n)][:], in1=bias_sb[:, cols], op=ALU.add
-                )
-                nc.scalar.activation(out=result[:, r, :], in_=result[:, r, :], func=ACT.Sigmoid)
-                nc.sync.dma_start(out=out_tokens[:, r, cols], in_=result[:, r, :])
+                result = results.tile([P, N_TILE], F32, name="result")
+                nc.vector.tensor_tensor(out=result[:], in0=sums[(r, n)][:], in1=bias_sb[:, cols], op=ALU.add)
+                sigmoids.append((result, out_tokens[:, r, cols]))
 
+        def sigmoid_next():
+            result, where = sigmoids[len(finished)]
+            finished.append(where)
+            nc.scalar.activation(out=result[:], in_=result[:], func=ACT.Sigmoid)
+            nc.sync.dma_start(out=where, in_=result[:])
+
+        done = []
+        started = []
+
+        def quantise(*pieces):
+            for w in pieces:
+                quantise_w(w)
+                done.append(w)
+                for r in started:
+                    multiply(r, w)
+
+        def start(r):
+            for w in done:
+                multiply(r, w)
+            started.append(r)
+
+        reduce_clean(0)
+        regroup_w(0)
+        reduce_rest(0)
+        regroup_w(1)
+        quantise(0)
         for r in range(TOKENS):
             turn_f1(r, 0)
-        for r in range(TOKENS):
             pack_f1(r, 0)
+        reduce_clean(1)
         for r in range(TOKENS):
             quantise_f1(r, 0)
-        multiplying = [0]
-        for l in range(W_LOADS + 1):
-            done = (2 * l - 2, 2 * l - 1) if l >= 1 else ()
-            if l < W_LOADS:
-                for w in (2 * l, 2 * l + 1):
-                    if w in TENSOR_PIECES:
-                        move_w(w)
-                    else:
-                        regroup_w(w)
-            for r in range(TOKENS):
-                if l == 2 * r + 2:
-                    pack_f1(r, 1)
-            for w in done:
-                quantise_w(w)
-            for r in range(TOKENS):
-                if l == 2 * r + 3:
-                    quantise_f1(r, 1)
-                    if r not in multiplying:
-                        for w in range(done[0]):
-                            multiply(r, w)
-                        multiplying.append(r)
-            for w in done:
-                for r in multiplying:
-                    multiply(r, w)
-            for w in done:
-                if w // N_TILES == PASSES - 1:
-                    finish(w % N_TILES)
-            if l < X2_LOADS:
-                reduce_x2(l)
-                if l % 2 == 1:
-                    turn_f1(l // 2, 1)
+        start(0)
+        quantise(1)
+        move_w(3)
+        regroup_w(2)
+        reduce_rest(1)
+        turn_f1(0, 1)
+        regroup_w(3)
+        pack_f1(0, 1)
+        reduce_clean(2)
+        quantise(2)
+        move_w(5)
+        regroup_w(4)
+        reduce_rest(2)
+        quantise_f1(0, 1)
+        quantise(3)
+        regroup_w(5)
+        reduce_clean(3)
+        move_w(7)
+        regroup_w(6)
+        quantise(4)
+        reduce_rest(3)
+        turn_f1(1, 1)
+        regroup_w(7)
+        quantise(5, 6)
+        regroup_w(8)
+        pack_f1(1, 1)
+        regroup_w(9)
+        quantise(7)
+        regroup_w(10)
+        regroup_w(11)
+        quantise(8)
+        quantise_f1(1, 1)
+        start(1)
+        quantise(9)
+        regroup_w(12)
+        quantise(10)
+        regroup_w(13)
+        quantise(11)
+        regroup_w(15)
+        quantise(12)
+        regroup_w(14)
+        quantise(13)
+        finish(0)
+        quantise(15)
+        finish(1)
+        quantise(14)
+        finish(3)
+        finish(2)
+        for i in range(8):
+            sigmoid_next()

@@ -15,6 +15,7 @@ P = 128
 PACK = 4
 SCENES = 16
 OBJECTS = 16
+HALF = OBJECTS // 2
 CH = 512
 PASSES = 4
 N_OUT = 2048
@@ -22,12 +23,11 @@ N_TILE = 512
 N_TILES = N_OUT // N_TILE
 TOKENS = 2
 SAME_SCENE = P // SCENES
-HALF = OBJECTS // 2
-X2_UNITS = tuple((r, h * HALF, HALF) for r in range(TOKENS) for h in range(2))
+X2_LOADS = 2 * TOKENS
 PIECES = PASSES * N_TILES
-SINGLE = 2
-TENSOR_PIECES = (3, 5, 7)
-VECTOR_PIECES = (9, 11, 13, 15)
+TENSOR_PIECES = (9, 10,)
+VECTOR_PIECES = (0, 13, 15,)
+EARLY = (0, 1)
 EXTREMES = (("max", ALU.max, 0.0), ("min", ALU.min, 1.0))
 
 FLOPS = 2 * SCENES * OBJECTS * PASSES * CH * N_OUT
@@ -43,8 +43,7 @@ def tile_differentiablelogicmachine_pb_kernel(tc, x0, x1, x2, W1, b1, out):
     with ExitStack() as ctx:
         ctx.enter_context(tc.manual_schedule())
         keep = ctx.enter_context(tc.tile_pool(name="keep", bufs=1))
-        stage = ctx.enter_context(tc.tile_pool(name="stage", bufs=8))
-        tree = ctx.enter_context(tc.tile_pool(name="tree", bufs=1))
+        stage = ctx.enter_context(tc.tile_pool(name="stage", bufs=5))
         results = ctx.enter_context(tc.tile_pool(name="results", bufs=8))
         psum = ctx.enter_context(tc.psum_pool(name="psum", bufs=1))
 
@@ -62,28 +61,25 @@ def tile_differentiablelogicmachine_pb_kernel(tc, x0, x1, x2, W1, b1, out):
         bias_sb = keep.tile([P, N_OUT], BF16)
         w_raw = {}
 
-        def piece(w):
-            return divmod(w, N_TILES)
-
         def load_w(w, count):
-            c, n = piece(w)
+            c, n = divmod(w, N_TILES)
             raw = keep.tile([P, PACK, count * N_TILE], BF16, name="w_raw_%d" % w)
             nc.sync.dma_start(out=raw[:], in_=w_rows[c][:, :, n * N_TILE : (n + count) * N_TILE])
             for i in range(count):
                 w_raw[w + i] = raw[:, :, i * N_TILE : (i + 1) * N_TILE]
 
-        x2_sb = [keep.tile([P, n, CH], BF16, name="x2_%d" % x) for x, (r, j, n) in enumerate(X2_UNITS)]
+        x2_sb = [keep.tile([P, HALF, CH], BF16, name="x2_%d" % x) for x in range(X2_LOADS)]
 
         def load_x2(x):
-            r, j, n = X2_UNITS[x]
-            nc.sync.dma_start(out=x2_sb[x][:], in_=x2_tokens[:, r, j : j + n, :])
+            r, h = divmod(x, 2)
+            nc.sync.dma_start(out=x2_sb[x][:], in_=x2_tokens[:, r, h * HALF : (h + 1) * HALF, :])
 
         def hide_diagonal(x):
-            r, j, n = X2_UNITS[x]
-            for i in range(j + r, j + n, TOKENS):
+            r, h = divmod(x, 2)
+            for i in range(h * HALF + r, (h + 1) * HALF, TOKENS):
                 neighbour = i + 1 - 2 * r
                 nc.sync.dma_start(
-                    out=x2_sb[x][i // TOKENS : P : SAME_SCENE, i - j, :],
+                    out=x2_sb[x][i // TOKENS : P : SAME_SCENE, i - h * HALF, :],
                     in_=x2[:, i, neighbour, :],
                 )
 
@@ -92,23 +88,34 @@ def tile_differentiablelogicmachine_pb_kernel(tc, x0, x1, x2, W1, b1, out):
         load_w(1, 1)
         hide_diagonal(0)
         load_x2(1)
+        load_w(2, 1)
         nc.sync.dma_start(out=x1_sb[:], in_=x1_tokens)
         nc.sync.dma_start(out=x0_rows[0:SCENES, :], in_=x0)
-        load_w(2, 2)
+        load_w(3, 1)
         hide_diagonal(1)
+        load_w(4, 1)
         load_x2(2)
-        load_w(4, 2)
+        load_w(5, 1)
+        load_w(6, 1)
         hide_diagonal(2)
         load_x2(3)
-        load_w(6, 2)
+        load_w(7, 1)
+        load_w(8, 1)
         hide_diagonal(3)
-        load_w(8, 4)
-        load_w(12, 4)
+        load_w(9, 1)
+        load_w(10, 2)
+        load_w(12, 2)
+        load_w(14, 2)
         nc.sync.dma_start(out=bias_sb[:], in_=b1.partition_broadcast(P))
 
         w_codes = keep.tile([P, PASSES, N_OUT], U32, align_bytes=64)
         w_scales = keep.tile([P, PASSES, N_OUT], U8, align_bytes=64)
-        w_grouped = {}
+        w_pairs = {}
+
+        def grouped(w):
+            if w // 2 not in w_pairs:
+                w_pairs[w // 2] = stage.tile([P, 2, N_TILE, PACK], BF16, name="w_pair", align_bytes=64)
+            return w_pairs[w // 2][:, w % 2]
 
         moved = {}
 
@@ -128,64 +135,83 @@ def tile_differentiablelogicmachine_pb_kernel(tc, x0, x1, x2, W1, b1, out):
                     )
 
         def regroup_w(w):
-            w_grouped[w] = stage.tile([P, N_TILE, PACK], BF16, name="w_grouped", align_bytes=64)
+            to = grouped(w)
             if w in TENSOR_PIECES:
+                half = N_TILE // 2
                 for side in range(2):
-                    half = N_TILE // 2
-                    nc.scalar.copy(out=w_grouped[w][:, side * half : (side + 1) * half, :], in_=moved[(w, side)][:])
+                    nc.scalar.copy(out=to[:, side * half : (side + 1) * half, :], in_=moved[(w, side)][:])
                 return
             copy = nc.vector.tensor_copy if w in VECTOR_PIECES else nc.scalar.copy
             copy(
-                out=w_grouped[w][:].rearrange("p (g i) t -> p g t i", i=4),
+                out=to.rearrange("p (g i) t -> p g t i", i=4),
                 in_=w_raw[w].rearrange("p t (g i) -> p g t i", i=4),
             )
 
-        def quantise_w(w):
-            c, n = piece(w)
-            cols = slice(n * N_TILE, (n + 1) * N_TILE)
-            nc.vector.quantize_mx(
-                out=w_codes[:, c, cols].bitcast(FP8X4),
-                scales=w_scales[:, c, cols],
-                in_=w_grouped[w][:].rearrange("p n t -> p (n t)"),
-            )
-
         run = {name: keep.tile([P, TOKENS, CH], BF16, name="run_" + name) for name, op, fill in EXTREMES}
+        four = {}
 
-        first_level = {}
+        def compare(out, in0, in1, op):
+            nc.vector.tensor_tensor(out=out, in0=in0, in1=in1, op=op)
 
         def reduce_clean(x):
-            r, j, n = X2_UNITS[x]
+            r, h = divmod(x, 2)
             for name, op, fill in EXTREMES:
-                level = tree.tile([P, 2, n // 4, CH], BF16, name="level_" + name)
-                first_level[(x, name)] = level
-                clean = x2_sb[x][:].rearrange("p (h k t) c -> p t h k c", h=2, t=TOKENS)[:, 1 - r]
-                nc.vector.tensor_tensor(out=level[:, 0], in0=clean[:, 0], in1=clean[:, 1], op=op)
+                four[(x, name)] = keep.tile([P, 4, CH], BF16, name="four_%d_%s" % (x % 2, name), tag="four_%d_%s" % (x % 2, name))
+                clean = x2_sb[x][:].rearrange("p (u k t) c -> p t u k c", u=2, t=TOKENS)[:, 1 - r]
+                compare(four[(x, name)][:, 0:2, :], clean[:, 0], clean[:, 1], op)
+            if x in EARLY:
+                for name, op, fill in EXTREMES:
+                    f = four[(x, name)]
+                    compare(f[:, 0, :], f[:, 0, :], f[:, 1, :], op)
 
         def reduce_rest(x):
-            r, j, n = X2_UNITS[x]
-            parts = {}
+            r, h = divmod(x, 2)
             for name, op, fill in EXTREMES:
-                level = first_level[(x, name)]
-                rest = x2_sb[x][:].rearrange("p (h k t) c -> p t h k c", h=2, t=TOKENS)[:, r]
-                nc.vector.tensor_tensor(out=level[:, 1], in0=rest[:, 0], in1=rest[:, 1], op=op)
-                parts[name] = level[:].rearrange("p u k c -> p (u k) c")
-            n //= 2
-            while n > 1:
-                n //= 2
+                rest = x2_sb[x][:].rearrange("p (u k t) c -> p t u k c", u=2, t=TOKENS)[:, r]
+                compare(four[(x, name)][:, 2:4, :], rest[:, 0], rest[:, 1], op)
+            if x in EARLY:
                 for name, op, fill in EXTREMES:
-                    level = tree.tile([P, n, CH], BF16, name="down_%d_%s" % (n, name))
-                    nc.vector.tensor_tensor(
-                        out=level[:], in0=parts[name][:, 0:n, :], in1=parts[name][:, n : 2 * n, :], op=op
-                    )
-                    parts[name] = level[:]
+                    f = four[(x, name)]
+                    compare(f[:, 2, :], f[:, 2, :], f[:, 3, :], op)
+                for name, op, fill in EXTREMES:
+                    f = four[(x, name)]
+                    if h == 0:
+                        compare(run[name][:, r, :], f[:, 0, :], f[:, 2, :], op)
+                    else:
+                        compare(f[:, 0, :], f[:, 0, :], f[:, 2, :], op)
+            else:
+                for name, op, fill in EXTREMES:
+                    f = four[(x, name)]
+                    compare(f[:, 0:2, :], f[:, 0:2, :], f[:, 2:4, :], op)
+                for name, op, fill in EXTREMES:
+                    f = four[(x, name)]
+                    compare(f[:, 0, :] if h == 1 else run[name][:, r, :], f[:, 0, :], f[:, 1, :], op)
+            if h == 1:
+                for name, op, fill in EXTREMES:
+                    compare(run[name][:, r, :], run[name][:, r, :], four[(x, name)][:, 0, :], op)
+
+        def reduce_whole(x):
+            r, h = divmod(x, 2)
             for name, op, fill in EXTREMES:
-                if j == 0:
+                four[(x, name)] = keep.tile([P, 4, CH], BF16, name="four_%d_%s" % (x % 2, name), tag="four_%d_%s" % (x % 2, name))
+                compare(four[(x, name)][:], x2_sb[x][:, 0:4, :], x2_sb[x][:, 4:8, :], op)
+
+        def fold(r):
+            for name, op, fill in EXTREMES:
+                f = four[(2 * r, name)]
+                compare(f[:], f[:], four[(2 * r + 1, name)][:], op)
+            for name, op, fill in EXTREMES:
+                f = four[(2 * r, name)]
+                compare(f[:, 0:2, :], f[:, 0:2, :], f[:, 2:4, :], op)
+            for name, op, fill in EXTREMES:
+                f = four[(2 * r, name)]
+                compare(run[name][:, r, :], f[:, 0, :], f[:, 1, :], op)
+
+        def fill_diagonal(r):
+            for name, op, fill in EXTREMES:
+                if name == "min" or not False:
                     nc.vector.tensor_scalar(
-                        out=run[name][:, r, :], in0=parts[name][:, 0, :], scalar1=fill, scalar2=None, op0=op
-                    )
-                else:
-                    nc.vector.tensor_tensor(
-                        out=run[name][:, r, :], in0=run[name][:, r, :], in1=parts[name][:, 0, :], op=op
+                        out=run[name][:, r, :], in0=run[name][:, r, :], scalar1=fill, scalar2=None, op0=op
                     )
 
         f1_codes = keep.tile([P, TOKENS, PASSES, P], U32, align_bytes=64)
@@ -218,6 +244,12 @@ def tile_differentiablelogicmachine_pb_kernel(tc, x0, x1, x2, W1, b1, out):
                         .unsqueeze(2)
                         .to_broadcast([P, SCENES, SAME_SCENE, 2]),
                     )
+                elif c == 2 and False:
+                    nc.scalar.activation(
+                        out=f1_grouped[r][:, c, :, :].rearrange("p m (u e) -> p m u e", u=2),
+                        in_=turned[(r, c)].bitcast(BF16).rearrange("p u (m e) -> p m u e", e=2),
+                        func=ACT.Relu,
+                    )
                 else:
                     nc.scalar.copy(out=words[:, c, :, :], in_=turned[(r, c)].rearrange("p u m -> p m u"))
 
@@ -233,7 +265,7 @@ def tile_differentiablelogicmachine_pb_kernel(tc, x0, x1, x2, W1, b1, out):
         sums = {}
 
         def multiply(r, w):
-            c, n = piece(w)
+            c, n = divmod(w, N_TILES)
             cols = slice(n * N_TILE, (n + 1) * N_TILE)
             if c == 0:
                 sums[(r, n)] = psum.tile([P, N_TILE], F32, tag="bank%d" % (4 * r + n), name="sums")
@@ -248,95 +280,107 @@ def tile_differentiablelogicmachine_pb_kernel(tc, x0, x1, x2, W1, b1, out):
                 stop=(c == PASSES - 1),
             )
 
-        sigmoids = []
-        finished = []
-
-        def finish(n):
-            cols = slice(n * N_TILE, (n + 1) * N_TILE)
-            for r in range(TOKENS):
-                result = results.tile([P, N_TILE], F32, name="result")
-                nc.vector.tensor_tensor(out=result[:], in0=sums[(r, n)][:], in1=bias_sb[:, cols], op=ALU.add)
-                sigmoids.append((result, out_tokens[:, r, cols]))
-
-        def sigmoid_next():
-            result, where = sigmoids[len(finished)]
-            finished.append(where)
-            nc.scalar.activation(out=result[:], in_=result[:], func=ACT.Sigmoid)
-            nc.sync.dma_start(out=where, in_=result[:])
-
         done = []
         started = []
 
-        def quantise(*pieces):
-            for w in pieces:
-                quantise_w(w)
-                done.append(w)
+        def quantise(w, count=1):
+            c, n = divmod(w, N_TILES)
+            cols = slice(n * N_TILE, (n + count) * N_TILE)
+            nc.vector.quantize_mx(
+                out=w_codes[:, c, cols].bitcast(FP8X4),
+                scales=w_scales[:, c, cols],
+                in_=w_pairs[w // 2][:, w % 2 : w % 2 + count].rearrange("p w n t -> p (w n t)"),
+            )
+            for i in range(count):
+                done.append(w + i)
                 for r in started:
-                    multiply(r, w)
+                    multiply(r, w + i)
 
         def start(r):
             for w in done:
                 multiply(r, w)
             started.append(r)
 
+        sigmoids = []
+        finished = []
+
+        def finish(n, parts=(1, 1)):
+            for r in range(TOKENS):
+                result = results.tile([P, N_TILE], F32, name="result")
+                width = N_TILE // parts[r]
+                for k in range(parts[r]):
+                    at = slice(k * width, (k + 1) * width)
+                    cols = slice(n * N_TILE + k * width, n * N_TILE + (k + 1) * width)
+                    nc.vector.tensor_tensor(out=result[:, at], in0=sums[(r, n)][:, at], in1=bias_sb[:, cols], op=ALU.add)
+                    sigmoids.append((result[:, at], out_tokens[:, r, cols]))
+
+        def sigmoid(count):
+            for i in range(count):
+                result, where = sigmoids[len(finished)]
+                finished.append(where)
+                nc.scalar.activation(out=result, in_=result, func=ACT.Sigmoid)
+                nc.sync.dma_start(out=where, in_=result)
+
         reduce_clean(0)
         regroup_w(0)
         reduce_rest(0)
         regroup_w(1)
         quantise(0)
-        for r in range(TOKENS):
-            turn_f1(r, 0)
-            pack_f1(r, 0)
-        reduce_clean(1)
-        for r in range(TOKENS):
-            quantise_f1(r, 0)
-        start(0)
-        quantise(1)
-        move_w(3)
         regroup_w(2)
-        reduce_rest(1)
-        turn_f1(0, 1)
+        quantise(1)
+        reduce_clean(1)
+        turn_f1(0, 0)
+        turn_f1(1, 0)
+        quantise(2)
         regroup_w(3)
+        pack_f1(0, 0)
+        pack_f1(1, 0)
+        reduce_rest(1)
+        fill_diagonal(0)
+        turn_f1(0, 1)
+        quantise_f1(0, 0)
+        quantise_f1(1, 0)
+        start(0)
+        quantise(3)
+        regroup_w(4)
         pack_f1(0, 1)
         reduce_clean(2)
-        quantise(2)
-        move_w(5)
-        regroup_w(4)
+        regroup_w(5)
+        quantise(4)
         reduce_rest(2)
         quantise_f1(0, 1)
-        quantise(3)
-        regroup_w(5)
-        reduce_clean(3)
-        move_w(7)
         regroup_w(6)
-        quantise(4)
-        reduce_rest(3)
-        turn_f1(1, 1)
+        quantise(5)
+        reduce_clean(3)
         regroup_w(7)
-        quantise(5, 6)
+        quantise(6)
+        move_w(9)
+        reduce_rest(3)
+        fill_diagonal(1)
+        turn_f1(1, 1)
+        move_w(10)
         regroup_w(8)
-        pack_f1(1, 1)
-        regroup_w(9)
         quantise(7)
-        regroup_w(10)
-        regroup_w(11)
+        regroup_w(9)
+        pack_f1(1, 1)
         quantise(8)
+        regroup_w(11)
+        quantise(9)
         quantise_f1(1, 1)
         start(1)
-        quantise(9)
-        regroup_w(12)
-        quantise(10)
         regroup_w(13)
         quantise(11)
-        regroup_w(15)
-        quantise(12)
-        regroup_w(14)
+        regroup_w(10)
         quantise(13)
-        finish(0)
+        quantise(10)
+        regroup_w(12)
+        regroup_w(15)
         quantise(15)
+        regroup_w(14)
+        quantise(12)
         finish(1)
-        quantise(14)
         finish(3)
+        quantise(14)
+        finish(0)
         finish(2)
-        for i in range(8):
-            sigmoid_next()
+        sigmoid(8)

@@ -25,7 +25,7 @@ TOKENS = 2
 SAME_SCENE = P // SCENES
 X2_LOADS = 2 * TOKENS
 PIECES = PASSES * N_TILES
-TENSOR_PIECES = (9, 10,)
+TENSOR_PIECES = ()
 VECTOR_PIECES = (0, 13, 15,)
 EARLY = (0, 1)
 EXTREMES = (("max", ALU.max, 0.0), ("min", ALU.min, 1.0))
@@ -145,6 +145,14 @@ def tile_differentiablelogicmachine_pb_kernel(tc, x0, x1, x2, W1, b1, out):
             copy(
                 out=to.rearrange("p (g i) t -> p g t i", i=4),
                 in_=w_raw[w].rearrange("p t (g i) -> p g t i", i=4),
+            )
+
+        def regroup_half(w, side, copy):
+            half = N_TILE // 2
+            cols = slice(side * half, (side + 1) * half)
+            copy(
+                out=grouped(w)[:, cols, :].rearrange("p (g i) t -> p g t i", i=4),
+                in_=w_raw[w][:, :, cols].rearrange("p t (g i) -> p g t i", i=4),
             )
 
         run = {name: keep.tile([P, TOKENS, CH], BF16, name="run_" + name) for name, op, fill in EXTREMES}
@@ -354,25 +362,24 @@ def tile_differentiablelogicmachine_pb_kernel(tc, x0, x1, x2, W1, b1, out):
         reduce_clean(3)
         regroup_w(7)
         quantise(6)
-        move_w(9)
         reduce_rest(3)
         fill_diagonal(1)
         turn_f1(1, 1)
-        move_w(10)
         regroup_w(8)
         quantise(7)
         regroup_w(9)
         pack_f1(1, 1)
         quantise(8)
-        regroup_w(11)
+        regroup_half(11, 0, nc.vector.tensor_copy)
         quantise(9)
         quantise_f1(1, 1)
         start(1)
         regroup_w(13)
-        quantise(11)
         regroup_w(10)
+        regroup_half(11, 1, nc.scalar.copy)
         quantise(13)
         quantise(10)
+        quantise(11)
         regroup_w(12)
         regroup_w(15)
         quantise(15)

@@ -15,7 +15,6 @@ P = 128
 PACK = 4
 SCENES = 16
 OBJECTS = 16
-HALF = OBJECTS // 2
 CH = 512
 PASSES = 4
 N_OUT = 2048
@@ -23,11 +22,10 @@ N_TILE = 512
 N_TILES = N_OUT // N_TILE
 TOKENS = 2
 SAME_SCENE = P // SCENES
-X2_LOADS = 2 * TOKENS
+HALF_J = OBJECTS // 2
 PIECES = PASSES * N_TILES
-TENSOR_PIECES = ()
-VECTOR_PIECES = (0, 13, 15,)
-EARLY = (0, 1)
+RUN = 4
+VECTOR_PIECES = (0, 11, 15)
 EXTREMES = (("max", ALU.max, 0.0), ("min", ALU.min, 1.0))
 
 FLOPS = 2 * SCENES * OBJECTS * PASSES * CH * N_OUT
@@ -44,13 +42,11 @@ def tile_differentiablelogicmachine_pb_kernel(tc, x0, x1, x2, W1, b1, out):
         ctx.enter_context(tc.manual_schedule())
         keep = ctx.enter_context(tc.tile_pool(name="keep", bufs=1))
         stage = ctx.enter_context(tc.tile_pool(name="stage", bufs=5))
-        results = ctx.enter_context(tc.tile_pool(name="results", bufs=8))
+        results = ctx.enter_context(tc.tile_pool(name="results", bufs=TOKENS * N_TILES))
         psum = ctx.enter_context(tc.psum_pool(name="psum", bufs=1))
 
         ident = keep.tile([P, P], F32)
         make_identity(nc, ident[:])
-        ident_bf = keep.tile([P, P], BF16)
-        make_identity(nc, ident_bf[:])
         x0_rows = keep.tile([P, CH], BF16)
         nc.vector.memset(x0_rows[:], 0.0)
         warm = keep.tile([P, 1], F32)
@@ -60,6 +56,7 @@ def tile_differentiablelogicmachine_pb_kernel(tc, x0, x1, x2, W1, b1, out):
         x1_sb = keep.tile([P, TOKENS, CH], BF16)
         bias_sb = keep.tile([P, N_OUT], BF16)
         w_raw = {}
+        x2_half = [keep.tile([P, HALF_J, CH], BF16, name="x2_half_%d" % x) for x in range(2 * TOKENS)]
 
         def load_w(w, count):
             c, n = divmod(w, N_TILES)
@@ -68,92 +65,57 @@ def tile_differentiablelogicmachine_pb_kernel(tc, x0, x1, x2, W1, b1, out):
             for i in range(count):
                 w_raw[w + i] = raw[:, :, i * N_TILE : (i + 1) * N_TILE]
 
-        x2_sb = [keep.tile([P, HALF, CH], BF16, name="x2_%d" % x) for x in range(X2_LOADS)]
-
         def load_x2(x):
             r, h = divmod(x, 2)
-            nc.sync.dma_start(out=x2_sb[x][:], in_=x2_tokens[:, r, h * HALF : (h + 1) * HALF, :])
+            nc.sync.dma_start(out=x2_half[x][:], in_=x2_tokens[:, r, h * HALF_J : (h + 1) * HALF_J, :])
 
-        def hide_diagonal(x):
+        def mend_x2(x):
             r, h = divmod(x, 2)
-            for i in range(h * HALF + r, (h + 1) * HALF, TOKENS):
-                neighbour = i + 1 - 2 * r
+            for i in range(h * HALF_J + r, (h + 1) * HALF_J, TOKENS):
                 nc.sync.dma_start(
-                    out=x2_sb[x][i // TOKENS : P : SAME_SCENE, i - h * HALF, :],
-                    in_=x2[:, i, neighbour, :],
+                    out=x2_half[x][i // TOKENS : P : SAME_SCENE, i - h * HALF_J, :],
+                    in_=x2[:, i, i + 1 - 2 * r, :],
                 )
 
         load_x2(0)
         load_w(0, 1)
         load_w(1, 1)
-        hide_diagonal(0)
+        mend_x2(0)
         load_x2(1)
         load_w(2, 1)
         nc.sync.dma_start(out=x1_sb[:], in_=x1_tokens)
         nc.sync.dma_start(out=x0_rows[0:SCENES, :], in_=x0)
         load_w(3, 1)
-        hide_diagonal(1)
+        mend_x2(1)
         load_w(4, 1)
         load_x2(2)
         load_w(5, 1)
         load_w(6, 1)
-        hide_diagonal(2)
+        mend_x2(2)
         load_x2(3)
         load_w(7, 1)
         load_w(8, 1)
-        hide_diagonal(3)
+        mend_x2(3)
         load_w(9, 1)
-        load_w(10, 2)
-        load_w(12, 2)
-        load_w(14, 2)
+        for w in range(10, PIECES, 2):
+            load_w(w, 2)
         nc.sync.dma_start(out=bias_sb[:], in_=b1.partition_broadcast(P))
 
         w_codes = keep.tile([P, PASSES, N_OUT], U32, align_bytes=64)
         w_scales = keep.tile([P, PASSES, N_OUT], U8, align_bytes=64)
         w_pairs = {}
 
-        def grouped(w):
+        def regroup(w, copy, cols=slice(0, N_TILE)):
             if w // 2 not in w_pairs:
                 w_pairs[w // 2] = stage.tile([P, 2, N_TILE, PACK], BF16, name="w_pair", align_bytes=64)
-            return w_pairs[w // 2][:, w % 2]
-
-        moved = {}
-
-        def move_w(w):
-            half = N_TILE // 2
-            for side in range(2):
-                moved[(w, side)] = psum.tile([P, half, PACK], BF16, tag="bank%d" % (4 + side), name="moved")
-                for q in range(2):
-                    cols = slice(q * half // 2, (q + 1) * half // 2)
-                    at = side * half + q * half // 2
-                    nc.tensor.matmul(
-                        out=moved[(w, side)][:, cols, :],
-                        lhsT=ident_bf[:],
-                        rhs=w_raw[w][:, :, at : at + half // 2].rearrange("p t n -> p n t"),
-                        start=True,
-                        stop=True,
-                    )
-
-        def regroup_w(w):
-            to = grouped(w)
-            if w in TENSOR_PIECES:
-                half = N_TILE // 2
-                for side in range(2):
-                    nc.scalar.copy(out=to[:, side * half : (side + 1) * half, :], in_=moved[(w, side)][:])
-                return
-            copy = nc.vector.tensor_copy if w in VECTOR_PIECES else nc.scalar.copy
             copy(
-                out=to.rearrange("p (g i) t -> p g t i", i=4),
-                in_=w_raw[w].rearrange("p t (g i) -> p g t i", i=4),
+                out=w_pairs[w // 2][:, w % 2, cols, :].rearrange("p (g i) t -> p g t i", i=RUN),
+                in_=w_raw[w][:, :, cols].rearrange("p t (g i) -> p g t i", i=RUN),
             )
 
-        def regroup_half(w, side, copy):
-            half = N_TILE // 2
-            cols = slice(side * half, (side + 1) * half)
-            copy(
-                out=grouped(w)[:, cols, :].rearrange("p (g i) t -> p g t i", i=4),
-                in_=w_raw[w][:, :, cols].rearrange("p t (g i) -> p g t i", i=4),
-            )
+        def regroup_w(*pieces):
+            for w in pieces:
+                regroup(w, nc.vector.tensor_copy if w in VECTOR_PIECES else nc.scalar.copy)
 
         run = {name: keep.tile([P, TOKENS, CH], BF16, name="run_" + name) for name, op, fill in EXTREMES}
         four = {}
@@ -161,63 +123,40 @@ def tile_differentiablelogicmachine_pb_kernel(tc, x0, x1, x2, W1, b1, out):
         def compare(out, in0, in1, op):
             nc.vector.tensor_tensor(out=out, in0=in0, in1=in1, op=op)
 
+        def entries(x, parity):
+            rows = x2_half[x][:].rearrange("p (u k t) c -> p t u k c", u=2, t=TOKENS)[:, parity]
+            return rows[:, 0], rows[:, 1]
+
         def reduce_clean(x):
-            r, h = divmod(x, 2)
+            r = x // 2
             for name, op, fill in EXTREMES:
-                four[(x, name)] = keep.tile([P, 4, CH], BF16, name="four_%d_%s" % (x % 2, name), tag="four_%d_%s" % (x % 2, name))
-                clean = x2_sb[x][:].rearrange("p (u k t) c -> p t u k c", u=2, t=TOKENS)[:, 1 - r]
-                compare(four[(x, name)][:, 0:2, :], clean[:, 0], clean[:, 1], op)
-            if x in EARLY:
+                four[(x, name)] = keep.tile(
+                    [P, 4, CH], BF16, name="four_%d_%s" % (x % 2, name), tag="four_%d_%s" % (x % 2, name)
+                )
+                compare(four[(x, name)][:, 0:2, :], *entries(x, 1 - r), op)
+            if r == 0:
                 for name, op, fill in EXTREMES:
-                    f = four[(x, name)]
-                    compare(f[:, 0, :], f[:, 0, :], f[:, 1, :], op)
+                    rows = four[(x, name)]
+                    compare(rows[:, 0, :], rows[:, 0, :], rows[:, 1, :], op)
 
         def reduce_rest(x):
             r, h = divmod(x, 2)
             for name, op, fill in EXTREMES:
-                rest = x2_sb[x][:].rearrange("p (u k t) c -> p t u k c", u=2, t=TOKENS)[:, r]
-                compare(four[(x, name)][:, 2:4, :], rest[:, 0], rest[:, 1], op)
-            if x in EARLY:
-                for name, op, fill in EXTREMES:
-                    f = four[(x, name)]
-                    compare(f[:, 2, :], f[:, 2, :], f[:, 3, :], op)
-                for name, op, fill in EXTREMES:
-                    f = four[(x, name)]
-                    if h == 0:
-                        compare(run[name][:, r, :], f[:, 0, :], f[:, 2, :], op)
-                    else:
-                        compare(f[:, 0, :], f[:, 0, :], f[:, 2, :], op)
-            else:
-                for name, op, fill in EXTREMES:
-                    f = four[(x, name)]
-                    compare(f[:, 0:2, :], f[:, 0:2, :], f[:, 2:4, :], op)
-                for name, op, fill in EXTREMES:
-                    f = four[(x, name)]
-                    compare(f[:, 0, :] if h == 1 else run[name][:, r, :], f[:, 0, :], f[:, 1, :], op)
+                compare(four[(x, name)][:, 2:4, :], *entries(x, r), op)
+            for name, op, fill in EXTREMES:
+                rows = four[(x, name)]
+                if r == 0:
+                    compare(rows[:, 2, :], rows[:, 2, :], rows[:, 3, :], op)
+                else:
+                    compare(rows[:, 0:2, :], rows[:, 0:2, :], rows[:, 2:4, :], op)
+            for name, op, fill in EXTREMES:
+                rows = four[(x, name)]
+                half = run[name][:, r, :] if h == 0 else rows[:, 0, :]
+                compare(half, rows[:, 0, :], rows[:, 2 if r == 0 else 1, :], op)
             if h == 1:
                 for name, op, fill in EXTREMES:
                     compare(run[name][:, r, :], run[name][:, r, :], four[(x, name)][:, 0, :], op)
-
-        def reduce_whole(x):
-            r, h = divmod(x, 2)
-            for name, op, fill in EXTREMES:
-                four[(x, name)] = keep.tile([P, 4, CH], BF16, name="four_%d_%s" % (x % 2, name), tag="four_%d_%s" % (x % 2, name))
-                compare(four[(x, name)][:], x2_sb[x][:, 0:4, :], x2_sb[x][:, 4:8, :], op)
-
-        def fold(r):
-            for name, op, fill in EXTREMES:
-                f = four[(2 * r, name)]
-                compare(f[:], f[:], four[(2 * r + 1, name)][:], op)
-            for name, op, fill in EXTREMES:
-                f = four[(2 * r, name)]
-                compare(f[:, 0:2, :], f[:, 0:2, :], f[:, 2:4, :], op)
-            for name, op, fill in EXTREMES:
-                f = four[(2 * r, name)]
-                compare(run[name][:, r, :], f[:, 0, :], f[:, 1, :], op)
-
-        def fill_diagonal(r):
-            for name, op, fill in EXTREMES:
-                if name == "min" or not False:
+                for name, op, fill in EXTREMES:
                     nc.vector.tensor_scalar(
                         out=run[name][:, r, :], in0=run[name][:, r, :], scalar1=fill, scalar2=None, op0=op
                     )
@@ -252,12 +191,6 @@ def tile_differentiablelogicmachine_pb_kernel(tc, x0, x1, x2, W1, b1, out):
                         .unsqueeze(2)
                         .to_broadcast([P, SCENES, SAME_SCENE, 2]),
                     )
-                elif c == 2 and False:
-                    nc.scalar.activation(
-                        out=f1_grouped[r][:, c, :, :].rearrange("p m (u e) -> p m u e", u=2),
-                        in_=turned[(r, c)].bitcast(BF16).rearrange("p u (m e) -> p m u e", e=2),
-                        func=ACT.Relu,
-                    )
                 else:
                     nc.scalar.copy(out=words[:, c, :, :], in_=turned[(r, c)].rearrange("p u m -> p m u"))
 
@@ -271,123 +204,110 @@ def tile_differentiablelogicmachine_pb_kernel(tc, x0, x1, x2, W1, b1, out):
             )
 
         sums = {}
+        quantised = []
+        multiplying = []
 
         def multiply(r, w):
             c, n = divmod(w, N_TILES)
             cols = slice(n * N_TILE, (n + 1) * N_TILE)
             if c == 0:
-                sums[(r, n)] = psum.tile([P, N_TILE], F32, tag="bank%d" % (4 * r + n), name="sums")
-            token = 0 if c == 0 else r
+                sums[(r, n)] = psum.tile([P, N_TILE], F32, tag="bank%d" % (r * N_TILES + n), name="sums")
+            of = 0 if c == 0 else r
             nc.tensor.matmul_mx(
                 out=sums[(r, n)][:],
-                lhsT=f1_codes[:, token, c, :].bitcast(FP8X4),
-                lhsT_scale=f1_scales[:, token, c, :],
+                lhsT=f1_codes[:, of, c, :].bitcast(FP8X4),
+                lhsT_scale=f1_scales[:, of, c, :],
                 rhs=w_codes[:, c, cols].bitcast(FP8X4),
                 rhs_scale=w_scales[:, c, cols],
                 start=(c == 0),
                 stop=(c == PASSES - 1),
             )
 
-        done = []
-        started = []
-
-        def quantise(w, count=1):
-            c, n = divmod(w, N_TILES)
-            cols = slice(n * N_TILE, (n + count) * N_TILE)
-            nc.vector.quantize_mx(
-                out=w_codes[:, c, cols].bitcast(FP8X4),
-                scales=w_scales[:, c, cols],
-                in_=w_pairs[w // 2][:, w % 2 : w % 2 + count].rearrange("p w n t -> p (w n t)"),
-            )
-            for i in range(count):
-                done.append(w + i)
-                for r in started:
-                    multiply(r, w + i)
-
-        def start(r):
-            for w in done:
+        def begin_products(r):
+            multiplying.append(r)
+            for w in quantised:
                 multiply(r, w)
-            started.append(r)
 
-        sigmoids = []
-        finished = []
+        def quantise_w(*pieces):
+            for w in pieces:
+                c, n = divmod(w, N_TILES)
+                cols = slice(n * N_TILE, (n + 1) * N_TILE)
+                nc.vector.quantize_mx(
+                    out=w_codes[:, c, cols].bitcast(FP8X4),
+                    scales=w_scales[:, c, cols],
+                    in_=w_pairs[w // 2][:, w % 2].rearrange("p n t -> p (n t)"),
+                )
+                quantised.append(w)
+                for r in multiplying:
+                    multiply(r, w)
 
-        def finish(n, parts=(1, 1)):
-            for r in range(TOKENS):
-                result = results.tile([P, N_TILE], F32, name="result")
-                width = N_TILE // parts[r]
-                for k in range(parts[r]):
-                    at = slice(k * width, (k + 1) * width)
-                    cols = slice(n * N_TILE + k * width, n * N_TILE + (k + 1) * width)
-                    nc.vector.tensor_tensor(out=result[:, at], in0=sums[(r, n)][:, at], in1=bias_sb[:, cols], op=ALU.add)
-                    sigmoids.append((result[:, at], out_tokens[:, r, cols]))
+        biased = []
 
-        def sigmoid(count):
-            for i in range(count):
-                result, where = sigmoids[len(finished)]
-                finished.append(where)
-                nc.scalar.activation(out=result, in_=result, func=ACT.Sigmoid)
-                nc.sync.dma_start(out=where, in_=result)
+        def add_bias(*tiles):
+            for n in tiles:
+                cols = slice(n * N_TILE, (n + 1) * N_TILE)
+                for r in range(TOKENS):
+                    result = results.tile([P, N_TILE], F32, name="result")
+                    nc.vector.tensor_tensor(out=result[:], in0=sums[(r, n)][:], in1=bias_sb[:, cols], op=ALU.add)
+                    biased.append((result, out_tokens[:, r, cols]))
 
         reduce_clean(0)
         regroup_w(0)
         reduce_rest(0)
         regroup_w(1)
-        quantise(0)
+        quantise_w(0)
         regroup_w(2)
-        quantise(1)
+        quantise_w(1)
         reduce_clean(1)
         turn_f1(0, 0)
         turn_f1(1, 0)
-        quantise(2)
+        quantise_w(2)
         regroup_w(3)
         pack_f1(0, 0)
         pack_f1(1, 0)
         reduce_rest(1)
-        fill_diagonal(0)
         turn_f1(0, 1)
         quantise_f1(0, 0)
         quantise_f1(1, 0)
-        start(0)
-        quantise(3)
+        begin_products(0)
+        quantise_w(3)
         regroup_w(4)
         pack_f1(0, 1)
         reduce_clean(2)
         regroup_w(5)
-        quantise(4)
+        quantise_w(4)
         reduce_rest(2)
         quantise_f1(0, 1)
         regroup_w(6)
-        quantise(5)
+        quantise_w(5)
         reduce_clean(3)
         regroup_w(7)
-        quantise(6)
+        quantise_w(6)
         reduce_rest(3)
-        fill_diagonal(1)
         turn_f1(1, 1)
         regroup_w(8)
-        quantise(7)
+        quantise_w(7)
         regroup_w(9)
         pack_f1(1, 1)
-        quantise(8)
-        regroup_half(11, 0, nc.vector.tensor_copy)
-        quantise(9)
+        quantise_w(8)
+        regroup_w(11)
+        quantise_w(9)
         quantise_f1(1, 1)
-        start(1)
-        regroup_w(13)
+        begin_products(1)
+        regroup(13, nc.vector.tensor_copy, slice(0, N_TILE // 2))
+        quantise_w(11)
         regroup_w(10)
-        regroup_half(11, 1, nc.scalar.copy)
-        quantise(13)
-        quantise(10)
-        quantise(11)
-        regroup_w(12)
+        regroup(13, nc.scalar.copy, slice(N_TILE // 2, N_TILE))
+        quantise_w(10)
         regroup_w(15)
-        quantise(15)
+        quantise_w(13)
+        regroup_w(12)
+        quantise_w(15)
         regroup_w(14)
-        quantise(12)
-        finish(1)
-        finish(3)
-        quantise(14)
-        finish(0)
-        finish(2)
-        sigmoid(8)
+        quantise_w(12)
+        add_bias(1, 3)
+        quantise_w(14)
+        add_bias(0, 2)
+        for result, where in biased:
+            nc.scalar.activation(out=result[:], in_=result[:], func=ACT.Sigmoid)
+            nc.sync.dma_start(out=where, in_=result[:])

from contextlib import ExitStack

import concourse.mybir as mybir
from concourse.masks import make_identity

BF16 = mybir.dt.bfloat16
F32 = mybir.dt.float32
U32 = mybir.dt.uint32
U8 = mybir.dt.uint8
FP8X4 = mybir.dt.float8_e4m3fn_x4
ALU = mybir.AluOpType
ACT = mybir.ActivationFunctionType

P = 128
PACK = 4
SCENES = 16
OBJECTS = 16
CH = 512
PASSES = 4
N_OUT = 2048
N_TILE = 512
N_TILES = N_OUT // N_TILE
TOKENS = 2
SAME_SCENE = P // SCENES
HALF_J = OBJECTS // 2
PIECES = PASSES * N_TILES
RUN = 4
VECTOR_PIECES = (0, 11, 15)
EXTREMES = (("max", ALU.max, 0.0), ("min", ALU.min, 1.0))

FLOPS = 2 * SCENES * OBJECTS * PASSES * CH * N_OUT


def tile_differentiablelogicmachine_pb_kernel(tc, x0, x1, x2, W1, b1, out):
    nc = tc.nc
    x1_tokens = x1.rearrange("b (s r) c -> (b s) r c", r=TOKENS)
    x2_tokens = x2.rearrange("b (s r) j c -> (b s) r j c", r=TOKENS)
    out_tokens = out.rearrange("b (s r) n -> (b s) r n", r=TOKENS)
    w_rows = W1.rearrange("(c p t) n -> c p t n", p=P, t=PACK)

    with ExitStack() as ctx:
        ctx.enter_context(tc.manual_schedule())
        keep = ctx.enter_context(tc.tile_pool(name="keep", bufs=1))
        stage = ctx.enter_context(tc.tile_pool(name="stage", bufs=5))
        results = ctx.enter_context(tc.tile_pool(name="results", bufs=TOKENS * N_TILES))
        psum = ctx.enter_context(tc.psum_pool(name="psum", bufs=1))

        ident = keep.tile([P, P], F32)
        make_identity(nc, ident[:])
        x0_rows = keep.tile([P, CH], BF16)
        nc.vector.memset(x0_rows[:], 0.0)
        warm = keep.tile([P, 1], F32)
        nc.vector.memset(warm[:], 0.0)
        nc.scalar.activation(out=warm[:], in_=warm[:], func=ACT.Sigmoid)

        x1_sb = keep.tile([P, TOKENS, CH], BF16)
        bias_sb = keep.tile([P, N_OUT], BF16)
        w_raw = {}
        x2_half = [keep.tile([P, HALF_J, CH], BF16, name="x2_half_%d" % x) for x in range(2 * TOKENS)]

        def load_w(w, count):
            c, n = divmod(w, N_TILES)
            raw = keep.tile([P, PACK, count * N_TILE], BF16, name="w_raw_%d" % w)
            nc.sync.dma_start(out=raw[:], in_=w_rows[c][:, :, n * N_TILE : (n + count) * N_TILE])
            for i in range(count):
                w_raw[w + i] = raw[:, :, i * N_TILE : (i + 1) * N_TILE]

        def load_x2(x):
            r, h = divmod(x, 2)
            nc.sync.dma_start(out=x2_half[x][:], in_=x2_tokens[:, r, h * HALF_J : (h + 1) * HALF_J, :])

        def mend_x2(x):
            r, h = divmod(x, 2)
            for i in range(h * HALF_J + r, (h + 1) * HALF_J, TOKENS):
                nc.sync.dma_start(
                    out=x2_half[x][i // TOKENS : P : SAME_SCENE, i - h * HALF_J, :],
                    in_=x2[:, i, i + 1 - 2 * r, :],
                )

        load_x2(0)
        load_w(0, 1)
        load_w(1, 1)
        mend_x2(0)
        load_x2(1)
        load_w(2, 1)
        nc.sync.dma_start(out=x1_sb[:], in_=x1_tokens)
        nc.sync.dma_start(out=x0_rows[0:SCENES, :], in_=x0)
        load_w(3, 1)
        mend_x2(1)
        load_w(4, 1)
        load_x2(2)
        load_w(5, 1)
        load_w(6, 1)
        mend_x2(2)
        load_x2(3)
        load_w(7, 1)
        load_w(8, 1)
        mend_x2(3)
        load_w(9, 1)
        for w in range(10, PIECES, 2):
            load_w(w, 2)
        nc.sync.dma_start(out=bias_sb[:], in_=b1.partition_broadcast(P))

        w_codes = keep.tile([P, PASSES, N_OUT], U32, align_bytes=64)
        w_scales = keep.tile([P, PASSES, N_OUT], U8, align_bytes=64)
        w_pairs = {}

        def regroup(w, copy, cols=slice(0, N_TILE)):
            if w // 2 not in w_pairs:
                w_pairs[w // 2] = stage.tile([P, 2, N_TILE, PACK], BF16, name="w_pair", align_bytes=64)
            copy(
                out=w_pairs[w // 2][:, w % 2, cols, :].rearrange("p (g i) t -> p g t i", i=RUN),
                in_=w_raw[w][:, :, cols].rearrange("p t (g i) -> p g t i", i=RUN),
            )

        def regroup_w(*pieces):
            for w in pieces:
                regroup(w, nc.vector.tensor_copy if w in VECTOR_PIECES else nc.scalar.copy)

        run = {name: keep.tile([P, TOKENS, CH], BF16, name="run_" + name) for name, op, fill in EXTREMES}
        four = {}

        def compare(out, in0, in1, op):
            nc.vector.tensor_tensor(out=out, in0=in0, in1=in1, op=op)

        def entries(x, parity):
            rows = x2_half[x][:].rearrange("p (u k t) c -> p t u k c", u=2, t=TOKENS)[:, parity]
            return rows[:, 0], rows[:, 1]

        def reduce_clean(x):
            r = x // 2
            for name, op, fill in EXTREMES:
                four[(x, name)] = keep.tile(
                    [P, 4, CH], BF16, name="four_%d_%s" % (x % 2, name), tag="four_%d_%s" % (x % 2, name)
                )
                compare(four[(x, name)][:, 0:2, :], *entries(x, 1 - r), op)
            if r == 0:
                for name, op, fill in EXTREMES:
                    rows = four[(x, name)]
                    compare(rows[:, 0, :], rows[:, 0, :], rows[:, 1, :], op)

        def reduce_rest(x):
            r, h = divmod(x, 2)
            for name, op, fill in EXTREMES:
                compare(four[(x, name)][:, 2:4, :], *entries(x, r), op)
            for name, op, fill in EXTREMES:
                rows = four[(x, name)]
                if r == 0:
                    compare(rows[:, 2, :], rows[:, 2, :], rows[:, 3, :], op)
                else:
                    compare(rows[:, 0:2, :], rows[:, 0:2, :], rows[:, 2:4, :], op)
            for name, op, fill in EXTREMES:
                rows = four[(x, name)]
                half = run[name][:, r, :] if h == 0 else rows[:, 0, :]
                compare(half, rows[:, 0, :], rows[:, 2 if r == 0 else 1, :], op)
            if h == 1:
                for name, op, fill in EXTREMES:
                    compare(run[name][:, r, :], run[name][:, r, :], four[(x, name)][:, 0, :], op)
                for name, op, fill in EXTREMES:
                    nc.vector.tensor_scalar(
                        out=run[name][:, r, :], in0=run[name][:, r, :], scalar1=fill, scalar2=None, op0=op
                    )

        f1_codes = keep.tile([P, TOKENS, PASSES, P], U32, align_bytes=64)
        f1_scales = keep.tile([P, TOKENS, PASSES, P], U8, align_bytes=64)
        f1_grouped = [
            keep.tile([P, PASSES, P, PACK], BF16, name="f1_grouped_%d" % r, align_bytes=64) for r in range(TOKENS)
        ]
        turned = {}

        def passes_of(r, part):
            return (1,) if (r, part) == (1, 0) else (2 * part, 2 * part + 1)

        def turn_f1(r, part):
            sources = (x0_rows[:], x1_sb[:, r, :], run["max"][:, r, :], run["min"][:, r, :])
            bank = psum.tile([P, 2, 2, P], F32, tag="bank%d" % (N_TILES + 2 * part + r), name="turned")
            for c in passes_of(r, part):
                turned[(r, c)] = bank[:, c % 2, :, :]
                words = sources[c].bitcast(F32)
                for u in range(2):
                    nc.tensor.transpose(turned[(r, c)][:, u, :], words[:, u : CH // 2 : 2], ident[:])

        def pack_f1(r, part):
            words = f1_grouped[r][:].bitcast(F32)
            for c in passes_of(r, part):
                if c == 0:
                    nc.scalar.copy(
                        out=words[:, c, :, :].rearrange("p (b g) u -> p b g u", g=SAME_SCENE),
                        in_=turned[(r, c)][:, :, 0:SCENES]
                        .rearrange("p u b -> p b u")
                        .unsqueeze(2)
                        .to_broadcast([P, SCENES, SAME_SCENE, 2]),
                    )
                else:
                    nc.scalar.copy(out=words[:, c, :, :], in_=turned[(r, c)].rearrange("p u m -> p m u"))

        def quantise_f1(r, part):
            c = passes_of(r, part)
            passes = slice(c[0], c[-1] + 1)
            nc.vector.quantize_mx(
                out=f1_codes[:, r, passes, :].rearrange("p c m -> p (c m)").bitcast(FP8X4),
                scales=f1_scales[:, r, passes, :].rearrange("p c m -> p (c m)"),
                in_=f1_grouped[r][:, passes, :, :].rearrange("p c m t -> p (c m t)"),
            )

        sums = {}
        quantised = []
        multiplying = []

        def multiply(r, w):
            c, n = divmod(w, N_TILES)
            cols = slice(n * N_TILE, (n + 1) * N_TILE)
            if c == 0:
                sums[(r, n)] = psum.tile([P, N_TILE], F32, tag="bank%d" % (r * N_TILES + n), name="sums")
            of = 0 if c == 0 else r
            nc.tensor.matmul_mx(
                out=sums[(r, n)][:],
                lhsT=f1_codes[:, of, c, :].bitcast(FP8X4),
                lhsT_scale=f1_scales[:, of, c, :],
                rhs=w_codes[:, c, cols].bitcast(FP8X4),
                rhs_scale=w_scales[:, c, cols],
                start=(c == 0),
                stop=(c == PASSES - 1),
            )

        def begin_products(r):
            multiplying.append(r)
            for w in quantised:
                multiply(r, w)

        def quantise_w(*pieces):
            for w in pieces:
                c, n = divmod(w, N_TILES)
                cols = slice(n * N_TILE, (n + 1) * N_TILE)
                nc.vector.quantize_mx(
                    out=w_codes[:, c, cols].bitcast(FP8X4),
                    scales=w_scales[:, c, cols],
                    in_=w_pairs[w // 2][:, w % 2].rearrange("p n t -> p (n t)"),
                )
                quantised.append(w)
                for r in multiplying:
                    multiply(r, w)

        biased = []

        def add_bias(*tiles):
            for n in tiles:
                cols = slice(n * N_TILE, (n + 1) * N_TILE)
                for r in range(TOKENS):
                    result = results.tile([P, N_TILE], F32, name="result")
                    nc.vector.tensor_tensor(out=result[:], in0=sums[(r, n)][:], in1=bias_sb[:, cols], op=ALU.add)
                    biased.append((result, out_tokens[:, r, cols]))

        reduce_clean(0)
        regroup_w(0)
        reduce_rest(0)
        regroup_w(1)
        quantise_w(0)
        regroup_w(2)
        quantise_w(1)
        reduce_clean(1)
        turn_f1(0, 0)
        turn_f1(1, 0)
        quantise_w(2)
        regroup_w(3)
        pack_f1(0, 0)
        pack_f1(1, 0)
        reduce_rest(1)
        turn_f1(0, 1)
        quantise_f1(0, 0)
        quantise_f1(1, 0)
        begin_products(0)
        quantise_w(3)
        regroup_w(4)
        pack_f1(0, 1)
        reduce_clean(2)
        regroup_w(5)
        quantise_w(4)
        reduce_rest(2)
        quantise_f1(0, 1)
        regroup_w(6)
        quantise_w(5)
        reduce_clean(3)
        regroup_w(7)
        quantise_w(6)
        reduce_rest(3)
        turn_f1(1, 1)
        regroup_w(8)
        quantise_w(7)
        regroup_w(9)
        pack_f1(1, 1)
        quantise_w(8)
        regroup_w(11)
        quantise_w(9)
        quantise_f1(1, 1)
        begin_products(1)
        regroup(13, nc.vector.tensor_copy, slice(0, N_TILE // 2))
        quantise_w(11)
        regroup_w(10)
        regroup(13, nc.scalar.copy, slice(N_TILE // 2, N_TILE))
        quantise_w(10)
        regroup_w(15)
        quantise_w(13)
        regroup_w(12)
        quantise_w(15)
        regroup_w(14)
        quantise_w(12)
        add_bias(1, 3)
        quantise_w(14)
        add_bias(0, 2)
        for result, where in biased:
            nc.scalar.activation(out=result[:], in_=result[:], func=ACT.Sigmoid)
            nc.sync.dma_start(out=where, in_=result[:])
